import numpy as np
import ml_dtypes


def mxq(x, axis, fmt="e4m3"):
    dtype, down = {"e4m3": (ml_dtypes.float8_e4m3fn, 7), "e5m2": (ml_dtypes.float8_e5m2, 14)}[fmt]
    v = np.moveaxis(np.asarray(x, np.float32).astype(ml_dtypes.bfloat16).astype(np.float64), axis, -1)
    blocks = v.reshape(v.shape[:-1] + (-1, 32))
    amax = np.abs(blocks).max(-1, keepdims=True)
    byte = np.maximum(np.where(amax > 0, np.frexp(amax)[1] - 1 + 127, 0) - down, 1)
    scale = np.exp2(byte - 127.0)
    codes = (blocks / scale).astype(np.float32).astype(dtype).astype(np.float64)
    return np.moveaxis((codes * scale).reshape(v.shape), -1, axis)


WIDE = False


def mx_kscale(k):
    if not WIDE:
        return np.ones(k)
    levels = np.array([10, -10, 5, -5, 0])
    a = np.random.permutation(np.resize(levels, k // 512 * 4)).reshape(k // 512, 4)
    idx = np.arange(k)
    return np.exp2(a[idx // 512, idx % 128 // 32])


BF16 = ml_dtypes.bfloat16


def bf(x):
    return np.asarray(x, np.float32).astype(BF16)


def f64(x):
    return np.asarray(x).astype(np.float64)


E2M1 = np.array([0.0, 0.5, 1.0, 1.5, 2.0, 3.0, 4.0, 6.0, -0.0, -0.5, -1.0, -1.5, -2.0, -3.0, -4.0, -6.0])


def pack_weight(w, fmt):
    k, n = w.shape
    w = f64(bf(w)).reshape(k // 32, 32, n)
    amax = np.abs(w).max(1)
    if fmt == "e4m3":
        byte = np.frexp(amax)[1] - 1 + 127 - 7
    else:
        mant, ex = np.frexp(amax / 6.0)
        byte = np.where(mant > 0.5, ex, ex - 1) + 127
    byte = np.clip(np.where(amax > 0, byte, 1), 1, 254)
    scaled = (w * np.exp2(127.0 - byte)[:, None, :]).reshape(k, n).astype(np.float32)
    by_word = np.ascontiguousarray(scaled.reshape(k // 512, 128, 4, n).transpose(0, 1, 3, 2))
    if fmt == "e4m3":
        words = by_word.astype(ml_dtypes.float8_e4m3fn).view(np.uint8)
    else:
        c = by_word.astype(ml_dtypes.float4_e2m1fn).view(np.uint8) & 0xF
        words = c[..., 0::2] | (c[..., 1::2] << 4)
    return np.ascontiguousarray(words), np.ascontiguousarray(byte.astype(np.uint8).reshape(k // 512, 16, n))


def unpack_weight(words, scales, fmt):
    g, p, n, _ = words.shape
    if fmt == "e4m3":
        vals = np.ascontiguousarray(words).view(ml_dtypes.float8_e4m3fn).astype(np.float64)
    else:
        nib = np.empty((g, p, n, 4), np.uint8)
        nib[..., 0::2] = words & 0xF
        nib[..., 1::2] = words >> 4
        vals = E2M1[nib]
    vals = vals * np.repeat(np.exp2(scales.astype(np.float64) - 127.0), 8, axis=1)[..., None]
    return vals.transpose(0, 1, 3, 2).reshape(g * 512, n)

def pack4(w):
    words, scales = pack_weight(w, "e2m1")
    return words.reshape(words.shape[0], 128, -1), scales


def unpack4(words, scales):
    return unpack_weight(words.reshape(words.shape[0], 128, -1, 2), scales, "e2m1")


N2, D, C, K = 2048, 1024, 512, 2048
EPSILON = 0.02
TEMPERATURE = 0.1
SINKHORN_ITERS = 3
RHO = 0.8
GAIN = 1.5


def log_softmax(v):
    v = v - v.max(axis=1, keepdims=True)
    return v - np.log(np.exp(v).sum(axis=1, keepdims=True))


def sinkhorn_knopp(z):
    Q = np.exp(z / EPSILON).T
    nk, nb = Q.shape
    Q = Q / Q.sum()
    for _ in range(SINKHORN_ITERS):
        Q = Q / (Q.sum(axis=1, keepdims=True) * nk)
        Q = Q / (Q.sum(axis=0, keepdims=True) * nb)
    Q = Q * nb
    return Q.T


def setup_inputs():
    s = mx_kscale(D)
    base = np.repeat(np.random.standard_normal((N2 // 2, D)), 2, axis=0)
    x = np.sqrt(RHO) * base + np.sqrt(1.0 - RHO) * np.random.standard_normal((N2, D))
    head_w = np.random.standard_normal((C, D)) / np.sqrt(D) / s
    head_w_words, head_w_scales = pack4(np.ascontiguousarray(head_w.T))
    return {"x": bf(x * s),
            "head_w_words": head_w_words,
            "head_w_scales": head_w_scales,
            "head_b": bf(np.random.standard_normal(C) * 0.5),
            "cb_v": bf(np.random.standard_normal((K, C)) / np.sqrt(C)),
            "cb_g": bf(GAIN * (1.0 + 0.1 * np.random.standard_normal(K)))}


def reference(x, head_w_words, head_w_scales, head_b, cb_v, cb_g):
    h = (mxq(f64(x), 1, "e4m3") @ unpack4(head_w_words, head_w_scales)) + f64(head_b)
    h = h / np.maximum(np.sqrt((h * h).sum(axis=1, keepdims=True)), 1e-12)
    v = f64(cb_v)
    w = f64(cb_g)[:, None] * v / np.sqrt((v * v).sum(axis=1, keepdims=True))
    z = mxq(h, 1, "e4m3") @ mxq(w, 1, "e4m3").T
    z1, z2 = z[::2], z[1::2]
    log_p1 = log_softmax(z1 / TEMPERATURE)
    log_p2 = log_softmax(z2 / TEMPERATURE)
    q1 = sinkhorn_knopp(z1)
    q2 = sinkhorn_knopp(z2)
    return -0.5 * ((q1 * log_p2).sum(axis=1) + (q2 * log_p1).sum(axis=1))

@@ -1,0 +1,427 @@
+from contextlib import ExitStack
+
+import concourse.mybir as mybir
+from concourse.masks import make_identity
+
+F32 = mybir.dt.float32
+BF16 = mybir.dt.bfloat16
+I32 = mybir.dt.int32
+U32 = mybir.dt.uint32
+U8 = mybir.dt.uint8
+FP8X4 = mybir.dt.float8_e4m3fn_x4
+FP4X4 = mybir.dt.float4_e2m1fn_x4
+ALU = mybir.AluOpType
+ACT = mybir.ActivationFunctionType
+AX = mybir.AxisListType
+
+P = 128
+PACK = 4
+BANK = 512
+VIEWS = 2
+D_IN = 1024
+PASSES_IN = D_IN // (P * PACK)
+D_EMB = 512
+SAMPLES = 1024
+S_TILES = SAMPLES // P
+CODES = 2048
+K_TILES = CODES // P
+ROW_TILES = VIEWS * S_TILES
+assert ROW_TILES == K_TILES
+GROUP = 4
+INV_EPSILON = 50.0
+INV_TEMPERATURE = 10.0
+MORE_ROUNDS = 2
+DIVIDE_LAG = 1
+ADD_LAG = 3
+CLOSE_LAG = 4
+
+FLOPS = 2 * VIEWS * SAMPLES * D_IN * D_EMB + 2 * VIEWS * SAMPLES * CODES * D_EMB
+
+
+def tile_spin_pa_kernel(tc, x, head_w_words, head_w_scales, head_b, cb_v, cb_g, out):
+    nc = tc.nc
+    with ExitStack() as ctx:
+        keep = ctx.enter_context(tc.tile_pool(name="keep", bufs=1))
+        small = ctx.enter_context(tc.tile_pool(name="small", bufs=4))
+        banks = ctx.enter_context(tc.psum_pool(name="banks", bufs=8))
+
+        ident_f32 = keep.tile([P, P], F32, name="ident_f32")
+        make_identity(nc, ident_f32[:])
+        ident_bf16 = keep.tile([P, P], BF16, name="ident_bf16")
+        make_identity(nc, ident_bf16[:])
+
+        hn_codes = keep.tile([P, VIEWS, SAMPLES], U32, name="hn_codes", align_bytes=64)
+        hn_scales = keep.tile([P, VIEWS, SAMPLES], U8, name="hn_scales", align_bytes=64)
+        w_codes = keep.tile([P, K_TILES, P], U32, name="w_codes", align_bytes=64)
+        w_scales = keep.tile([P, K_TILES, P], U8, name="w_scales", align_bytes=64)
+
+        with tc.tile_pool(name="stage", bufs=3) as stage, tc.tile_pool(name="inputs", bufs=1) as inputs:
+            w4_scales = inputs.tile([P, PASSES_IN, D_EMB], U8, name="w4_scales", align_bytes=64)
+            nc.vector.memset(w4_scales[:].bitcast(I32), 0)
+            for quadrant in range(4):
+                nc.sync.dma_start(
+                    out=w4_scales[32 * quadrant : 32 * quadrant + 4, :, :].bitcast(I32),
+                    in_=head_w_scales.bitcast(I32)[:, 4 * quadrant : 4 * quadrant + 4, :].rearrange("g r n -> r g n"),
+                )
+            w4_words = inputs.tile([P, PASSES_IN, 2 * D_EMB], U8, name="w4_words", align_bytes=64)
+            nc.sync.dma_start(out=w4_words[:].bitcast(I32), in_=head_w_words.bitcast(I32).rearrange("g p b -> p g b"))
+
+            x_sb = inputs.tile([P, VIEWS, S_TILES, D_IN], BF16, name="x_sb")
+            x_rows = x.rearrange("(p t v) d -> v p t d", t=S_TILES, v=VIEWS)
+            cb_sb = inputs.tile([P, K_TILES, D_EMB], BF16, name="cb_sb")
+            cb_rows = cb_v.rearrange("(p t) c -> p t c", t=K_TILES)
+            gain = inputs.tile([P, K_TILES], BF16, name="gain")
+            bias_row = inputs.tile([P, D_EMB], BF16, name="bias_row")
+
+            for first in range(0, ROW_TILES, GROUP):
+                view, t = first // S_TILES, first % S_TILES
+                nc.sync.dma_start(out=x_sb[:, view, t : t + GROUP, :], in_=x_rows[view][:, t : t + GROUP, :])
+                if first == 0:
+                    nc.sync.dma_start(out=bias_row[:], in_=head_b.partition_broadcast(P))
+                    nc.sync.dma_start(out=gain[:], in_=cb_g.rearrange("(p t) -> p t", t=K_TILES))
+                nc.sync.dma_start(out=cb_sb[:, first : first + GROUP, :], in_=cb_rows[:, first : first + GROUP, :])
+
+            h_rows = inputs.tile([P, ROW_TILES, D_EMB], F32, name="h_rows")
+            h_square_sum = inputs.tile([P, ROW_TILES], F32, name="h_square_sum")
+            v_square_sum = inputs.tile([P, K_TILES], F32, name="v_square_sum")
+            x_turned = {}
+            x_grouped = {}
+            x_quantised = {}
+            h_sums = {}
+            norms = {}
+            normalised = {}
+            factors = {}
+            grouped = {}
+            turned = {}
+
+            def turn_x(i):
+                x_words = x_sb[:, i // S_TILES, i % S_TILES, :].bitcast(F32)
+                x_turned[i] = banks.tile([P, PASSES_IN, 2, P], F32, tag="bank", name="x_turned")
+                for g in range(PASSES_IN):
+                    for u in range(2):
+                        nc.tensor.transpose(
+                            x_turned[i][:, g, u, :], x_words[:, 256 * g + u : 256 * (g + 1) : 2], ident_f32[:]
+                        )
+
+            def lay_out_x(i):
+                x_grouped[i] = stage.tile([P, PASSES_IN, P, PACK], BF16, name="x_grouped", align_bytes=64)
+                nc.scalar.copy(out=x_grouped[i][:].bitcast(F32), in_=x_turned[i][:].rearrange("p g u s -> p g s u"))
+
+            def quantise_x(i):
+                x_codes = stage.tile([P, PASSES_IN, P], U32, name="x_codes", align_bytes=64)
+                x_scales = stage.tile([P, PASSES_IN, P], U8, name="x_scales", align_bytes=64)
+                nc.vector.quantize_mx(
+                    out=x_codes[:].rearrange("p g s -> p (g s)").bitcast(FP8X4),
+                    scales=x_scales[:].rearrange("p g s -> p (g s)"),
+                    in_=x_grouped[i][:].rearrange("p g s j -> p (g s j)"),
+                )
+                x_quantised[i] = (x_codes, x_scales)
+
+            def multiply_by_head(i):
+                x_codes, x_scales = x_quantised[i]
+                h_sums[i] = banks.tile([P, D_EMB], F32, tag="bank", name="h_sum")
+                for g in range(PASSES_IN):
+                    nc.tensor.matmul_mx(
+                        out=h_sums[i][:],
+                        lhsT=x_codes[:, g, :].bitcast(FP8X4),
+                        lhsT_scale=x_scales[:, g, :],
+                        rhs=w4_words[:, g, :].bitcast(FP4X4),
+                        rhs_scale=w4_scales[:, g, :],
+                        start=(g == 0),
+                        stop=(g == PASSES_IN - 1),
+                    )
+
+            def add_bias(i):
+                nc.vector.tensor_tensor(out=h_rows[:, i, :], in0=h_sums[i][:], in1=bias_row[:], op=ALU.add)
+
+            def square_rows(i):
+                for rows, square_sum in ((h_rows[:, i, :], h_square_sum), (cb_sb[:, i, :], v_square_sum)):
+                    squares = stage.tile([P, D_EMB], BF16, name="squares")
+                    nc.scalar.activation(out=squares[:], in_=rows, func=ACT.Square, accum_out=square_sum[:, i : i + 1])
+                if i % GROUP == GROUP - 1:
+                    tiles = slice(i + 1 - GROUP, i + 1)
+                    h_norm = small.tile([P, GROUP], F32, name="h_norm")
+                    nc.scalar.sqrt(out=h_norm[:], in_=h_square_sum[:, tiles])
+                    v_norm = small.tile([P, GROUP], F32, name="v_norm")
+                    nc.scalar.sqrt(out=v_norm[:], in_=v_square_sum[:, tiles])
+                    norms[i + 1 - GROUP] = (h_norm, v_norm)
+
+            def factors_of_group(first):
+                h_norm, v_norm = norms[first]
+                nc.vector.tensor_scalar_max(out=h_norm[:], in0=h_norm[:], scalar1=1e-12)
+                inv_h = small.tile([P, GROUP], F32, name="inv_h")
+                nc.vector.reciprocal(out=inv_h[:], in_=h_norm[:])
+                inv_v = small.tile([P, GROUP], F32, name="inv_v")
+                nc.vector.reciprocal(out=inv_v[:], in_=v_norm[:])
+                nc.vector.tensor_tensor(out=inv_v[:], in0=inv_v[:], in1=gain[:, first : first + GROUP], op=ALU.mult)
+                factors[first] = (inv_h, inv_v)
+                grouped[first] = (
+                    stage.tile([P, GROUP, P, PACK], BF16, name="hn_grouped", align_bytes=64),
+                    stage.tile([P, GROUP, P, PACK], BF16, name="w_grouped", align_bytes=64),
+                )
+
+            def normalise(i):
+                inv_h, gain_over_v = factors[i - i % GROUP]
+                slot = i % GROUP
+                hn_rows = stage.tile([P, D_EMB], BF16, name="hn_rows")
+                nc.vector.tensor_scalar_mul(out=hn_rows[:], in0=h_rows[:, i, :], scalar1=inv_h[:, slot : slot + 1])
+                w_rows = stage.tile([P, D_EMB], BF16, name="w_rows")
+                nc.vector.tensor_scalar_mul(out=w_rows[:], in0=cb_sb[:, i, :], scalar1=gain_over_v[:, slot : slot + 1])
+                normalised[i] = (hn_rows, w_rows)
+
+            def turn_rows(i):
+                turned[i] = []
+                for rows in normalised[i]:
+                    columns = banks.tile([P, PACK, P], BF16, tag="bank", name="columns")
+                    for j in range(PACK):
+                        nc.tensor.transpose(columns[:, j, :], rows[:, j * P : (j + 1) * P], ident_bf16[:])
+                    turned[i].append(columns)
+
+            def lay_out_rows(i):
+                hn_grouped, w_grouped = grouped[i - i % GROUP]
+                hn_columns, w_columns = turned[i]
+                slot = i % GROUP
+                nc.scalar.copy(out=hn_grouped[:, slot, :, :], in_=hn_columns[:].rearrange("p j r -> p r j"))
+                nc.vector.tensor_copy(out=w_grouped[:, slot, :, :], in_=w_columns[:].rearrange("p j r -> p r j"))
+
+            def quantise_group(first):
+                hn_grouped, w_grouped = grouped[first]
+                view, t = first // S_TILES, first % S_TILES
+                nc.vector.quantize_mx(
+                    out=hn_codes[:, view, t * P : (t + GROUP) * P].bitcast(FP8X4),
+                    scales=hn_scales[:, view, t * P : (t + GROUP) * P],
+                    in_=hn_grouped[:].rearrange("p t s j -> p (t s j)"),
+                )
+                nc.vector.quantize_mx(
+                    out=w_codes[:, first : first + GROUP, :].rearrange("p t k -> p (t k)").bitcast(FP8X4),
+                    scales=w_scales[:, first : first + GROUP, :].rearrange("p t k -> p (t k)"),
+                    in_=w_grouped[:].rearrange("p t k j -> p (t k j)"),
+                )
+
+            to_the_norms = (turn_x, lay_out_x, quantise_x, multiply_by_head, add_bias, square_rows)
+            from_the_norms = (normalise, turn_rows, lay_out_rows)
+            factors_lag = len(to_the_norms) + GROUP - 1
+            quantise_lag = factors_lag + len(from_the_norms) + GROUP
+            with tc.manual_schedule():
+                for now in range(ROW_TILES - GROUP + quantise_lag + 1):
+                    if 0 <= now - quantise_lag < ROW_TILES and (now - quantise_lag) % GROUP == 0:
+                        quantise_group(now - quantise_lag)
+                    for lag, step in reversed(list(enumerate(from_the_norms))):
+                        if 0 <= now - factors_lag - 1 - lag < ROW_TILES:
+                            step(now - factors_lag - 1 - lag)
+                    if 0 <= now - factors_lag < ROW_TILES and (now - factors_lag) % GROUP == 0:
+                        factors_of_group(now - factors_lag)
+                    for lag, step in reversed(list(enumerate(to_the_norms))):
+                        if 0 <= now - lag < ROW_TILES:
+                            step(now - lag)
+
+        matrix = ctx.enter_context(tc.tile_pool(name="matrix", bufs=1))
+        work = ctx.enter_context(tc.tile_pool(name="work", bufs=2))
+        e = [matrix.tile([P, K_TILES, SAMPLES], F32, name="e%d" % view) for view in range(VIEWS)]
+
+        def logits_by_code(kt, view, half):
+            zt = banks.tile([P, BANK], F32, tag="bank")
+            columns = slice(half * BANK, (half + 1) * BANK)
+            nc.tensor.matmul_mx(
+                out=zt[:],
+                lhsT=w_codes[:, kt, :].bitcast(FP8X4),
+                lhsT_scale=w_scales[:, kt, :],
+                rhs=hn_codes[:, view, columns].bitcast(FP8X4),
+                rhs_scale=hn_scales[:, view, columns],
+                start=True,
+                stop=True,
+            )
+            return zt, columns
+
+        def new_sample_sums():
+            return [banks.tile([P, GROUP, P], F32, tag="bank", name="added%d" % i) for i in range(S_TILES // GROUP)]
+
+        def add_code_tile(added, view, kt, last_kt):
+            for t in range(S_TILES):
+                nc.tensor.matmul(
+                    out=added[t // GROUP][:, t % GROUP, :], lhsT=e[view][:, kt, t * P : (t + 1) * P], rhs=ident_f32[:],
+                    is_transpose=True,
+                    start=(kt == 0 and t % GROUP == 0), stop=(kt == last_kt and t % GROUP == GROUP - 1),
+                )
+
+        def finish_sample_sums(added):
+            sums = small.tile([P, S_TILES], F32, name="sums", bufs=8)
+            for i, bank in enumerate(added):
+                nc.vector.tensor_reduce(out=sums[:, i * GROUP : (i + 1) * GROUP], in_=bank[:], axis=AX.X, op=ALU.add)
+            return sums
+
+        units = []
+        for view in range(VIEWS):
+            units.extend([("exp", view, first, "weigh") for first in range(0, K_TILES, GROUP)])
+        for rounds_left in reversed(range(MORE_ROUNDS)):
+            for view in range(VIEWS):
+                then = "weigh" if rounds_left > 0 else "dot"
+                units.extend([("weigh", view, first, then) for first in range(0, K_TILES, GROUP)])
+        for view in range(VIEWS):
+            units.extend([("dot", view, first, "end") for first in range(0, K_TILES, GROUP)])
+        first_weigh_unit = VIEWS * K_TILES // GROUP
+
+        shift = keep.tile([P, VIEWS, K_TILES], F32, name="shift")
+        soft_shift = keep.tile([P, 1], F32, name="soft_shift")
+        exp_part = keep.tile([P, VIEWS, S_TILES, CODES // BANK], F32, name="exp_part")
+        part_sums = {}
+        added = [None, None]
+        weight_row = [None, None]
+        last_sum = [None, None]
+        dot_sum = [None, None]
+
+        def start_tile(number, slot):
+            kind, view, first, then = units[number]
+            if kind != "dot" and slot == 0:
+                part_sums[number] = small.tile([P, GROUP, 2], F32, name="part_sum", bufs=4)
+            kt = first + slot
+            if kind == "exp":
+                halves = [logits_by_code(kt, view, half) for half in range(2)]
+                top = small.tile([P, 2], F32, name="top")
+                for half, (zt, columns) in enumerate(halves):
+                    nc.vector.tensor_reduce(out=top[:, half : half + 1], in_=zt[:], axis=AX.X, op=ALU.max)
+                nc.vector.tensor_scalar(
+                    out=shift[:, view, kt : kt + 1], in0=top[:, 0:1], scalar1=top[:, 1:2], scalar2=-INV_EPSILON,
+                    op0=ALU.max, op1=ALU.mult,
+                )
+                for half, (zt, columns) in enumerate(halves):
+                    nc.scalar.activation(
+                        out=e[view][:, kt, columns], in_=zt[:], func=ACT.Exp,
+                        bias=shift[:, view, kt : kt + 1], scale=INV_EPSILON,
+                        accum_out=part_sums[number][:, slot, half : half + 1],
+                    )
+            elif kind == "weigh":
+                for half in range(2):
+                    products = work.tile([P, BANK], F32, name="products")
+                    nc.vector.scalar_tensor_tensor(
+                        out=products[:], in0=e[view][:, kt, half * BANK : (half + 1) * BANK], scalar=1.0,
+                        in1=weight_row[view][half][:].rearrange("p t m -> p (t m)"), op0=ALU.mult, op1=ALU.mult,
+                        accum_out=part_sums[number][:, slot, half : half + 1],
+                    )
+            else:
+                for half in range(2):
+                    zt, columns = logits_by_code(kt, 1 - view, half)
+                    nc.vector.tensor_tensor(
+                        out=e[view][:, kt, columns], in0=zt[:], in1=e[view][:, kt, columns], op=ALU.mult
+                    )
+
+        def divide_unit(number):
+            kind, view, first, then = units[number]
+            if kind == "dot":
+                for kt in range(first, first + GROUP, 2):
+                    nc.gpsimd.tensor_tensor(out=e[view][:, kt, :], in0=e[view][:, kt, :], in1=e[view][:, kt + 1, :], op=ALU.add)
+                return
+            code_sum = small.tile([P, GROUP], F32, name="code_sum")
+            nc.vector.tensor_reduce(out=code_sum[:], in_=part_sums[number][:], axis=AX.X, op=ALU.add)
+            inv_code = small.tile([P, GROUP], F32, name="inv_code")
+            nc.vector.reciprocal(out=inv_code[:], in_=code_sum[:])
+            for slot in range(GROUP):
+                kt = first + slot
+                if kind == "weigh" and kt % 2 == 0:
+                    nc.scalar.activation(
+                        out=e[view][:, kt, :], in_=e[view][:, kt, :], func=ACT.Copy, scale=inv_code[:, slot : slot + 1]
+                    )
+                else:
+                    nc.gpsimd.tensor_scalar(
+                        out=e[view][:, kt, :], in0=e[view][:, kt, :], scalar1=inv_code[:, slot : slot + 1], scalar2=0.0,
+                        op0=ALU.mult, op1=ALU.add,
+                    )
+
+        def softmax_piece(piece):
+            chunk = piece % (CODES // BANK)
+            t = (piece // (CODES // BANK)) % S_TILES
+            view = piece // (CODES // BANK * S_TILES)
+            z = banks.tile([P, BANK], F32, tag="bank")
+            tiles = slice(chunk * GROUP, (chunk + 1) * GROUP)
+            nc.tensor.matmul_mx(
+                out=z[:],
+                lhsT=hn_codes[:, view, t * P : (t + 1) * P].bitcast(FP8X4),
+                lhsT_scale=hn_scales[:, view, t * P : (t + 1) * P],
+                rhs=w_codes[:, tiles, :].rearrange("p t k -> p (t k)").bitcast(FP8X4),
+                rhs_scale=w_scales[:, tiles, :].rearrange("p t k -> p (t k)"),
+                start=True,
+                stop=True,
+            )
+            powers = work.tile([P, BANK], BF16, name="powers")
+            nc.scalar.activation(
+                out=powers[:], in_=z[:], func=ACT.Exp, bias=soft_shift[:], scale=INV_TEMPERATURE,
+                accum_out=exp_part[:, view, t, chunk : chunk + 1],
+            )
+
+        def add_tile_of_unit(number, slot):
+            kind, view, first, then = units[number]
+            if first + slot == 0:
+                added[view] = new_sample_sums()
+            if kind != "dot":
+                add_code_tile(added[view], view, first + slot, K_TILES - 1)
+            elif slot % 2 == 0:
+                add_code_tile(added[view], view, first + slot, K_TILES - 2)
+
+        def close_pass(number):
+            kind, view, first, then = units[number]
+            if first != K_TILES - GROUP:
+                return
+            sums = finish_sample_sums(added[view])
+            if then == "dot":
+                last_sum[view] = sums
+            elif then == "end":
+                dot_sum[view] = sums
+            else:
+                weight = small.tile([P, S_TILES], F32, name="weight")
+                nc.vector.reciprocal(out=weight[:], in_=sums[:])
+                weight_row[view] = [banks.tile([P, GROUP, P], F32, tag="bank", name="row%d" % i) for i in range(2)]
+                for t in range(S_TILES):
+                    nc.tensor.transpose(
+                        weight_row[view][t // GROUP][:, t % GROUP, :], weight[:, t : t + 1].to_broadcast([P, P]),
+                        ident_f32[:],
+                    )
+
+        def make_soft_shift():
+            least = small.tile([P, 1], F32, name="least")
+            nc.vector.tensor_reduce(out=least[:], in_=shift[:].rearrange("p v k -> p (v k)"), axis=AX.X, op=ALU.min)
+            least_turned = banks.tile([P, P], F32, tag="bank")
+            nc.tensor.transpose(least_turned[:], least[:].to_broadcast([P, P]), ident_f32[:])
+            least_of_all = small.tile([P, 1], F32, name="least_of_all")
+            nc.vector.tensor_reduce(out=least_of_all[:], in_=least_turned[:], axis=AX.X, op=ALU.min)
+            nc.vector.tensor_scalar_mul(out=soft_shift[:], in0=least_of_all[:], scalar1=INV_TEMPERATURE / INV_EPSILON)
+
+        with tc.manual_schedule():
+            for now in range(len(units) + CLOSE_LAG):
+                if 0 <= now - CLOSE_LAG:
+                    close_pass(now - CLOSE_LAG)
+                if now == first_weigh_unit:
+                    make_soft_shift()
+                for slot in range(GROUP):
+                    if now < len(units):
+                        start_tile(now, slot)
+                    if 0 <= now - ADD_LAG < len(units):
+                        add_tile_of_unit(now - ADD_LAG, slot)
+                    if now < len(units) and units[now][0] == "weigh":
+                        softmax_piece((now - first_weigh_unit) * GROUP + slot)
+                if 0 <= now - DIVIDE_LAG < len(units):
+                    divide_unit(now - DIVIDE_LAG)
+
+        exp_sum = small.tile([P, VIEWS, S_TILES], F32, name="exp_sum")
+        nc.vector.tensor_reduce(out=exp_sum[:], in_=exp_part[:], axis=AX.X, op=ALU.add)
+        log_sum = small.tile([P, VIEWS, S_TILES], F32, name="log_sum")
+        nc.scalar.activation(out=log_sum[:], in_=exp_sum[:], func=ACT.Ln)
+
+        mean_logit = []
+        for view in range(VIEWS):
+            inv_last = small.tile([P, S_TILES], F32, name="inv_last")
+            nc.vector.reciprocal(out=inv_last[:], in_=last_sum[view][:])
+            ratio = small.tile([P, S_TILES], F32, name="ratio")
+            nc.vector.tensor_tensor(out=ratio[:], in0=dot_sum[view][:], in1=inv_last[:], op=ALU.mult)
+            mean_logit.append(ratio)
+        both_logits = small.tile([P, S_TILES], F32, name="both_logits")
+        nc.vector.tensor_tensor(out=both_logits[:], in0=mean_logit[0][:], in1=mean_logit[1][:], op=ALU.add)
+        both_logs = small.tile([P, S_TILES], F32, name="both_logs")
+        nc.vector.tensor_tensor(out=both_logs[:], in0=log_sum[:, 0, :], in1=log_sum[:, 1, :], op=ALU.add)
+        nc.vector.tensor_scalar(
+            out=both_logs[:], in0=both_logs[:], scalar1=0.5, scalar2=soft_shift[:], op0=ALU.mult, op1=ALU.subtract
+        )
+        loss = small.tile([P, S_TILES], F32, name="loss")
+        nc.vector.scalar_tensor_tensor(
+            out=loss[:], in0=both_logits[:], scalar=-0.5 * INV_TEMPERATURE, in1=both_logs[:], op0=ALU.mult, op1=ALU.add
+        )
+        nc.sync.dma_start(out=out.rearrange("(p t) -> p t", t=S_TILES), in_=loss[:])

@@ -149,10 +149,10 @@ def tile_spin_pa_kernel(tc, x, head_w_words, head_w_scales, head_b, cb_v, cb_g, 
             def factors_of_group(first):
                 h_norm, v_norm = norms[first]
                 nc.vector.tensor_scalar_max(out=h_norm[:], in0=h_norm[:], scalar1=1e-12)
-                inv_h = small.tile([P, GROUP], F32, name="inv_h")
-                nc.vector.reciprocal(out=inv_h[:], in_=h_norm[:])
                 inv_v = small.tile([P, GROUP], F32, name="inv_v")
                 nc.vector.reciprocal(out=inv_v[:], in_=v_norm[:])
+                inv_h = small.tile([P, GROUP], F32, name="inv_h")
+                nc.vector.reciprocal(out=inv_h[:], in_=h_norm[:])
                 nc.vector.tensor_tensor(out=inv_v[:], in0=inv_v[:], in1=gain[:, first : first + GROUP], op=ALU.mult)
                 factors[first] = (inv_h, inv_v)
                 grouped[first] = (
@@ -270,16 +270,12 @@ def tile_spin_pa_kernel(tc, x, head_w_words, head_w_scales, head_b, cb_v, cb_g, 
         last_sum = [None, None]
         dot_sum = [None, None]
 
-        def start_tile(number, slot):
-            kind, view, first, then = units[number]
-            if kind != "dot" and slot == 0:
-                part_sums[number] = small.tile([P, GROUP, 2], F32, name="part_sum", bufs=4)
-            kt = first + slot
-            if kind == "exp":
-                halves = [logits_by_code(kt, view, half) for half in range(2)]
-                top = small.tile([P, 2], F32, name="top")
-                for half, (zt, columns) in enumerate(halves):
-                    nc.vector.tensor_reduce(out=top[:, half : half + 1], in_=zt[:], axis=AX.X, op=ALU.max)
+        waiting_exp = []
+
+        def exp_of_waiting_tile():
+            for number, slot, halves, top in waiting_exp:
+                kind, view, first, then = units[number]
+                kt = first + slot
                 nc.vector.tensor_scalar(
                     out=shift[:, view, kt : kt + 1], in0=top[:, 0:1], scalar1=top[:, 1:2], scalar2=-INV_EPSILON,
                     op0=ALU.max, op1=ALU.mult,
@@ -290,6 +286,21 @@ def tile_spin_pa_kernel(tc, x, head_w_words, head_w_scales, head_b, cb_v, cb_g, 
                         bias=shift[:, view, kt : kt + 1], scale=INV_EPSILON,
                         accum_out=part_sums[number][:, slot, half : half + 1],
                     )
+            waiting_exp.clear()
+
+        def start_tile(number, slot, small_steps):
+            kind, view, first, then = units[number]
+            if kind != "dot" and slot == 0:
+                part_sums[number] = small.tile([P, GROUP, 2], F32, name="part_sum", bufs=4)
+            kt = first + slot
+            if kind == "exp":
+                halves = [logits_by_code(kt, view, half) for half in range(2)]
+                top = small.tile([P, 2], F32, name="top")
+                for half, (zt, columns) in enumerate(halves):
+                    nc.vector.tensor_reduce(out=top[:, half : half + 1], in_=zt[:], axis=AX.X, op=ALU.max)
+                    if half == 0:
+                        small_steps()
+                waiting_exp.append((number, slot, halves, top))
             elif kind == "weigh":
                 for half in range(2):
                     products = work.tile([P, BANK], F32, name="products")
@@ -298,12 +309,29 @@ def tile_spin_pa_kernel(tc, x, head_w_words, head_w_scales, head_b, cb_v, cb_g, 
                         in1=weight_row[view][half][:].rearrange("p t m -> p (t m)"), op0=ALU.mult, op1=ALU.mult,
                         accum_out=part_sums[number][:, slot, half : half + 1],
                     )
+                    if half == 0:
+                        small_steps()
             else:
                 for half in range(2):
                     zt, columns = logits_by_code(kt, 1 - view, half)
                     nc.vector.tensor_tensor(
                         out=e[view][:, kt, columns], in0=zt[:], in1=e[view][:, kt, columns], op=ALU.mult
                     )
+                    if half == 0:
+                        small_steps()
+
+        code_sums = {}
+        inv_codes = {}
+
+        def add_halves(number):
+            if units[number][0] != "dot":
+                code_sums[number] = small.tile([P, GROUP], F32, name="code_sum")
+                nc.vector.tensor_reduce(out=code_sums[number][:], in_=part_sums[number][:], axis=AX.X, op=ALU.add)
+
+        def invert_sums(number):
+            if units[number][0] != "dot":
+                inv_codes[number] = small.tile([P, GROUP], F32, name="inv_code")
+                nc.vector.reciprocal(out=inv_codes[number][:], in_=code_sums[number][:])
 
         def divide_unit(number):
             kind, view, first, then = units[number]
@@ -311,10 +339,7 @@ def tile_spin_pa_kernel(tc, x, head_w_words, head_w_scales, head_b, cb_v, cb_g, 
                 for kt in range(first, first + GROUP, 2):
                     nc.gpsimd.tensor_tensor(out=e[view][:, kt, :], in0=e[view][:, kt, :], in1=e[view][:, kt + 1, :], op=ALU.add)
                 return
-            code_sum = small.tile([P, GROUP], F32, name="code_sum")
-            nc.vector.tensor_reduce(out=code_sum[:], in_=part_sums[number][:], axis=AX.X, op=ALU.add)
-            inv_code = small.tile([P, GROUP], F32, name="inv_code")
-            nc.vector.reciprocal(out=inv_code[:], in_=code_sum[:])
+            inv_code = inv_codes[number]
             for slot in range(GROUP):
                 kt = first + slot
                 if kind == "weigh" and kt % 2 == 0:
@@ -367,6 +392,12 @@ def tile_spin_pa_kernel(tc, x, head_w_words, head_w_scales, head_b, cb_v, cb_g, 
             elif then == "end":
                 dot_sum[view] = sums
             else:
+                waiting_weights.append((view, sums))
+
+        waiting_weights = []
+
+        def weights_of_waiting_view():
+            for view, sums in waiting_weights:
                 weight = small.tile([P, S_TILES], F32, name="weight")
                 nc.vector.reciprocal(out=weight[:], in_=sums[:])
                 weight_row[view] = [banks.tile([P, GROUP, P], F32, tag="bank", name="row%d" % i) for i in range(2)]
@@ -375,6 +406,7 @@ def tile_spin_pa_kernel(tc, x, head_w_words, head_w_scales, head_b, cb_v, cb_g, 
                         weight_row[view][t // GROUP][:, t % GROUP, :], weight[:, t : t + 1].to_broadcast([P, P]),
                         ident_f32[:],
                     )
+            waiting_weights.clear()
 
         def make_soft_shift():
             least = small.tile([P, 1], F32, name="least")
@@ -385,43 +417,68 @@ def tile_spin_pa_kernel(tc, x, head_w_words, head_w_scales, head_b, cb_v, cb_g, 
             nc.vector.tensor_reduce(out=least_of_all[:], in_=least_turned[:], axis=AX.X, op=ALU.min)
             nc.vector.tensor_scalar_mul(out=soft_shift[:], in0=least_of_all[:], scalar1=INV_TEMPERATURE / INV_EPSILON)
 
+        def small_steps_of(now, slot):
+            def small_steps():
+                exp_of_waiting_tile()
+                if slot == 0:
+                    weights_of_waiting_view()
+                if slot == GROUP - 1 and 0 <= now - DIVIDE_LAG < len(units):
+                    add_halves(now - DIVIDE_LAG)
+
+            return small_steps
+
+        log_sum = small.tile([P, VIEWS, S_TILES], F32, name="log_sum")
+        inv_last = [small.tile([P, S_TILES], F32, name="inv_last%d" % view) for view in range(VIEWS)]
+        all_but_last = small.tile([P, S_TILES], F32, name="all_but_last")
+
+        def take_logarithms():
+            exp_sum = small.tile([P, VIEWS, S_TILES], F32, name="exp_sum")
+            nc.vector.tensor_reduce(out=exp_sum[:], in_=exp_part[:], axis=AX.X, op=ALU.add)
+            nc.scalar.activation(out=log_sum[:], in_=exp_sum[:], func=ACT.Ln)
+
+        def all_but_the_last_term():
+            both_logs = small.tile([P, S_TILES], F32, name="both_logs")
+            nc.vector.tensor_tensor(out=both_logs[:], in0=log_sum[:, 0, :], in1=log_sum[:, 1, :], op=ALU.add)
+            for view in range(VIEWS):
+                nc.vector.reciprocal(out=inv_last[view][:], in_=last_sum[view][:])
+            nc.vector.tensor_scalar(
+                out=both_logs[:], in0=both_logs[:], scalar1=0.5, scalar2=soft_shift[:], op0=ALU.mult, op1=ALU.subtract
+            )
+            first_logit = small.tile([P, S_TILES], F32, name="first_logit")
+            nc.vector.tensor_tensor(out=first_logit[:], in0=dot_sum[0][:], in1=inv_last[0][:], op=ALU.mult)
+            nc.vector.scalar_tensor_tensor(
+                out=all_but_last[:], in0=first_logit[:], scalar=-0.5 * INV_TEMPERATURE, in1=both_logs[:],
+                op0=ALU.mult, op1=ALU.add,
+            )
+
         with tc.manual_schedule():
             for now in range(len(units) + CLOSE_LAG):
+                if now == len(units):
+                    take_logarithms()
+                if now == len(units) + CLOSE_LAG - 1:
+                    all_but_the_last_term()
                 if 0 <= now - CLOSE_LAG:
                     close_pass(now - CLOSE_LAG)
                 if now == first_weigh_unit:
+                    exp_of_waiting_tile()
                     make_soft_shift()
                 for slot in range(GROUP):
                     if now < len(units):
-                        start_tile(now, slot)
+                        start_tile(now, slot, small_steps_of(now, slot))
+                    else:
+                        small_steps_of(now, slot)()
                     if 0 <= now - ADD_LAG < len(units):
                         add_tile_of_unit(now - ADD_LAG, slot)
                     if now < len(units) and units[now][0] == "weigh":
                         softmax_piece((now - first_weigh_unit) * GROUP + slot)
                 if 0 <= now - DIVIDE_LAG < len(units):
+                    invert_sums(now - DIVIDE_LAG)
                     divide_unit(now - DIVIDE_LAG)
 
-        exp_sum = small.tile([P, VIEWS, S_TILES], F32, name="exp_sum")
-        nc.vector.tensor_reduce(out=exp_sum[:], in_=exp_part[:], axis=AX.X, op=ALU.add)
-        log_sum = small.tile([P, VIEWS, S_TILES], F32, name="log_sum")
-        nc.scalar.activation(out=log_sum[:], in_=exp_sum[:], func=ACT.Ln)
-
-        mean_logit = []
-        for view in range(VIEWS):
-            inv_last = small.tile([P, S_TILES], F32, name="inv_last")
-            nc.vector.reciprocal(out=inv_last[:], in_=last_sum[view][:])
-            ratio = small.tile([P, S_TILES], F32, name="ratio")
-            nc.vector.tensor_tensor(out=ratio[:], in0=dot_sum[view][:], in1=inv_last[:], op=ALU.mult)
-            mean_logit.append(ratio)
-        both_logits = small.tile([P, S_TILES], F32, name="both_logits")
-        nc.vector.tensor_tensor(out=both_logits[:], in0=mean_logit[0][:], in1=mean_logit[1][:], op=ALU.add)
-        both_logs = small.tile([P, S_TILES], F32, name="both_logs")
-        nc.vector.tensor_tensor(out=both_logs[:], in0=log_sum[:, 0, :], in1=log_sum[:, 1, :], op=ALU.add)
-        nc.vector.tensor_scalar(
-            out=both_logs[:], in0=both_logs[:], scalar1=0.5, scalar2=soft_shift[:], op0=ALU.mult, op1=ALU.subtract
-        )
-        loss = small.tile([P, S_TILES], F32, name="loss")
-        nc.vector.scalar_tensor_tensor(
-            out=loss[:], in0=both_logits[:], scalar=-0.5 * INV_TEMPERATURE, in1=both_logs[:], op0=ALU.mult, op1=ALU.add
-        )
-        nc.sync.dma_start(out=out.rearrange("(p t) -> p t", t=S_TILES), in_=loss[:])
+            last_logit = small.tile([P, S_TILES], F32, name="last_logit")
+            nc.vector.tensor_tensor(out=last_logit[:], in0=dot_sum[1][:], in1=inv_last[1][:], op=ALU.mult)
+            loss = small.tile([P, S_TILES], F32, name="loss")
+            nc.vector.scalar_tensor_tensor(
+                out=loss[:], in0=last_logit[:], scalar=-0.5 * INV_TEMPERATURE, in1=all_but_last[:], op0=ALU.mult, op1=ALU.add
+            )
+            nc.sync.dma_start(out=out.rearrange("(p t) -> p t", t=S_TILES), in_=loss[:])

@@ -47,8 +47,6 @@ def tile_spin_pa_kernel(tc, x, head_w_words, head_w_scales, head_b, cb_v, cb_g, 
 
         ident_f32 = keep.tile([P, P], F32, name="ident_f32")
         make_identity(nc, ident_f32[:])
-        ident_bf16 = keep.tile([P, P], BF16, name="ident_bf16")
-        make_identity(nc, ident_bf16[:])
 
         hn_codes = keep.tile([P, VIEWS, SAMPLES], U32, name="hn_codes", align_bytes=64)
         hn_scales = keep.tile([P, VIEWS, SAMPLES], U8, name="hn_scales", align_bytes=64)
@@ -56,6 +54,9 @@ def tile_spin_pa_kernel(tc, x, head_w_words, head_w_scales, head_b, cb_v, cb_g, 
         w_scales = keep.tile([P, K_TILES, P], U8, name="w_scales", align_bytes=64)
 
         with tc.tile_pool(name="stage", bufs=3) as stage, tc.tile_pool(name="inputs", bufs=1) as inputs:
+            x_sb = inputs.tile([P, VIEWS, S_TILES, D_IN], BF16, name="x_sb")
+            x_rows = x.rearrange("(p t v) d -> v p t d", t=S_TILES, v=VIEWS)
+            nc.sync.dma_start(out=x_sb[:, 0, 0:1, :], in_=x_rows[0][:, 0:1, :])
             w4_scales = inputs.tile([P, PASSES_IN, D_EMB], U8, name="w4_scales", align_bytes=64)
             nc.vector.memset(w4_scales[:].bitcast(I32), 0)
             for quadrant in range(4):
@@ -66,8 +67,6 @@ def tile_spin_pa_kernel(tc, x, head_w_words, head_w_scales, head_b, cb_v, cb_g, 
             w4_words = inputs.tile([P, PASSES_IN, 2 * D_EMB], U8, name="w4_words", align_bytes=64)
             nc.sync.dma_start(out=w4_words[:].bitcast(I32), in_=head_w_words.bitcast(I32).rearrange("g p b -> p g b"))
 
-            x_sb = inputs.tile([P, VIEWS, S_TILES, D_IN], BF16, name="x_sb")
-            x_rows = x.rearrange("(p t v) d -> v p t d", t=S_TILES, v=VIEWS)
             cb_sb = inputs.tile([P, K_TILES, D_EMB], BF16, name="cb_sb")
             cb_rows = cb_v.rearrange("(p t) c -> p t c", t=K_TILES)
             gain = inputs.tile([P, K_TILES], BF16, name="gain")
@@ -75,7 +74,8 @@ def tile_spin_pa_kernel(tc, x, head_w_words, head_w_scales, head_b, cb_v, cb_g, 
 
             for first in range(0, ROW_TILES, GROUP):
                 view, t = first // S_TILES, first % S_TILES
-                nc.sync.dma_start(out=x_sb[:, view, t : t + GROUP, :], in_=x_rows[view][:, t : t + GROUP, :])
+                loaded = 1 if first == 0 else 0
+                nc.sync.dma_start(out=x_sb[:, view, t + loaded : t + GROUP, :], in_=x_rows[view][:, t + loaded : t + GROUP, :])
                 if first == 0:
                     nc.sync.dma_start(out=bias_row[:], in_=head_b.partition_broadcast(P))
                     nc.sync.dma_start(out=gain[:], in_=cb_g.rearrange("(p t) -> p t", t=K_TILES))
@@ -172,17 +172,18 @@ def tile_spin_pa_kernel(tc, x, head_w_words, head_w_scales, head_b, cb_v, cb_g, 
             def turn_rows(i):
                 turned[i] = []
                 for rows in normalised[i]:
-                    columns = banks.tile([P, PACK, P], BF16, tag="bank", name="columns")
-                    for j in range(PACK):
-                        nc.tensor.transpose(columns[:, j, :], rows[:, j * P : (j + 1) * P], ident_bf16[:])
+                    words = rows[:].bitcast(F32)
+                    columns = banks.tile([P, 2, P], F32, tag="bank", name="columns")
+                    for u in range(2):
+                        nc.tensor.transpose(columns[:, u, :], words[:, u * P : (u + 1) * P], ident_f32[:])
                     turned[i].append(columns)
 
             def lay_out_rows(i):
                 hn_grouped, w_grouped = grouped[i - i % GROUP]
                 hn_columns, w_columns = turned[i]
                 slot = i % GROUP
-                nc.scalar.copy(out=hn_grouped[:, slot, :, :], in_=hn_columns[:].rearrange("p j r -> p r j"))
-                nc.vector.tensor_copy(out=w_grouped[:, slot, :, :], in_=w_columns[:].rearrange("p j r -> p r j"))
+                nc.scalar.copy(out=hn_grouped[:, slot, :, :].bitcast(F32), in_=hn_columns[:].rearrange("p u r -> p r u"))
+                nc.vector.tensor_copy(out=w_grouped[:, slot, :, :].bitcast(F32), in_=w_columns[:].rearrange("p u r -> p r u"))
 
             def quantise_group(first):
                 hn_grouped, w_grouped = grouped[first]
@@ -336,8 +337,11 @@ def tile_spin_pa_kernel(tc, x, head_w_words, head_w_scales, head_b, cb_v, cb_g, 
         def divide_unit(number):
             kind, view, first, then = units[number]
             if kind == "dot":
-                for kt in range(first, first + GROUP, 2):
-                    nc.gpsimd.tensor_tensor(out=e[view][:, kt, :], in0=e[view][:, kt, :], in1=e[view][:, kt + 1, :], op=ALU.add)
+                if number < len(units) - 1:
+                    for kt in range(first, first + GROUP, 2):
+                        nc.gpsimd.tensor_tensor(
+                            out=e[view][:, kt, :], in0=e[view][:, kt, :], in1=e[view][:, kt + 1, :], op=ALU.add
+                        )
                 return
             inv_code = inv_codes[number]
             for slot in range(GROUP):
@@ -377,10 +381,10 @@ def tile_spin_pa_kernel(tc, x, head_w_words, head_w_scales, head_b, cb_v, cb_g, 
             kind, view, first, then = units[number]
             if first + slot == 0:
                 added[view] = new_sample_sums()
-            if kind != "dot":
+            if kind != "dot" or number == len(units) - 1:
                 add_code_tile(added[view], view, first + slot, K_TILES - 1)
             elif slot % 2 == 0:
-                add_code_tile(added[view], view, first + slot, K_TILES - 2)
+                add_code_tile(added[view], view, first + slot, K_TILES - 1 if view == VIEWS - 1 else K_TILES - 2)
 
         def close_pass(number):
             kind, view, first, then = units[number]

@@ -34,6 +34,7 @@ MORE_ROUNDS = 2
 DIVIDE_LAG = 1
 ADD_LAG = 3
 CLOSE_LAG = 4
+RUN = 2
 
 FLOPS = 2 * VIEWS * SAMPLES * D_IN * D_EMB + 2 * VIEWS * SAMPLES * CODES * D_EMB
 
@@ -261,6 +262,7 @@ def tile_spin_pa_kernel(tc, x, head_w_words, head_w_scales, head_b, cb_v, cb_g, 
         for view in range(VIEWS):
             units.extend([("dot", view, first, "end") for first in range(0, K_TILES, GROUP)])
         first_weigh_unit = VIEWS * K_TILES // GROUP
+        SOFTMAX_PIECES = VIEWS * S_TILES * (CODES // BANK)
 
         shift = keep.tile([P, VIEWS, K_TILES], F32, name="shift")
         soft_shift = keep.tile([P, 1], F32, name="soft_shift")
@@ -412,20 +414,27 @@ def tile_spin_pa_kernel(tc, x, head_w_words, head_w_scales, head_b, cb_v, cb_g, 
                     )
             waiting_weights.clear()
 
-        def make_soft_shift():
-            least = small.tile([P, 1], F32, name="least")
-            nc.vector.tensor_reduce(out=least[:], in_=shift[:].rearrange("p v k -> p (v k)"), axis=AX.X, op=ALU.min)
-            least_turned = banks.tile([P, P], F32, tag="bank")
-            nc.tensor.transpose(least_turned[:], least[:].to_broadcast([P, P]), ident_f32[:])
-            least_of_all = small.tile([P, 1], F32, name="least_of_all")
-            nc.vector.tensor_reduce(out=least_of_all[:], in_=least_turned[:], axis=AX.X, op=ALU.min)
-            nc.vector.tensor_scalar_mul(out=soft_shift[:], in0=least_of_all[:], scalar1=INV_TEMPERATURE / INV_EPSILON)
+        least = small.tile([P, 1], F32, name="least")
+        least_of_all = small.tile([P, 1], F32, name="least_of_all")
+        least_turned = []
+
+        def soft_shift_step(step):
+            if step == 1:
+                nc.vector.tensor_reduce(out=least[:], in_=shift[:].rearrange("p v k -> p (v k)"), axis=AX.X, op=ALU.min)
+                least_turned.append(banks.tile([P, P], F32, tag="bank", name="least_turned"))
+                nc.tensor.transpose(least_turned[0][:], least[:].to_broadcast([P, P]), ident_f32[:])
+            elif step == 2:
+                nc.vector.tensor_reduce(out=least_of_all[:], in_=least_turned[0][:], axis=AX.X, op=ALU.min)
+            elif step == 3:
+                nc.vector.tensor_scalar_mul(out=soft_shift[:], in0=least_of_all[:], scalar1=INV_TEMPERATURE / INV_EPSILON)
 
         def small_steps_of(now, slot):
             def small_steps():
                 exp_of_waiting_tile()
-                if slot == 0:
+                if slot == GROUP - 2:
                     weights_of_waiting_view()
+                if now == first_weigh_unit:
+                    soft_shift_step(slot)
                 if slot == GROUP - 1 and 0 <= now - DIVIDE_LAG < len(units):
                     add_halves(now - DIVIDE_LAG)
 
@@ -463,18 +472,17 @@ def tile_spin_pa_kernel(tc, x, head_w_words, head_w_scales, head_b, cb_v, cb_g, 
                     all_but_the_last_term()
                 if 0 <= now - CLOSE_LAG:
                     close_pass(now - CLOSE_LAG)
-                if now == first_weigh_unit:
-                    exp_of_waiting_tile()
-                    make_soft_shift()
-                for slot in range(GROUP):
-                    if now < len(units):
-                        start_tile(now, slot, small_steps_of(now, slot))
-                    else:
-                        small_steps_of(now, slot)()
-                    if 0 <= now - ADD_LAG < len(units):
-                        add_tile_of_unit(now - ADD_LAG, slot)
-                    if now < len(units) and units[now][0] == "weigh":
-                        softmax_piece((now - first_weigh_unit) * GROUP + slot)
+                for first_slot in range(0, GROUP, RUN):
+                    for slot in range(first_slot, first_slot + RUN):
+                        if now < len(units):
+                            start_tile(now, slot, small_steps_of(now, slot))
+                        else:
+                            small_steps_of(now, slot)()
+                        if first_weigh_unit < now <= first_weigh_unit + SOFTMAX_PIECES // GROUP:
+                            softmax_piece((now - first_weigh_unit - 1) * GROUP + slot)
+                    for slot in range(first_slot, first_slot + RUN):
+                        if 0 <= now - ADD_LAG < len(units):
+                            add_tile_of_unit(now - ADD_LAG, slot)
                 if 0 <= now - DIVIDE_LAG < len(units):
                     invert_sums(now - DIVIDE_LAG)
                     divide_unit(now - DIVIDE_LAG)

@@ -67,18 +67,23 @@ def tile_spin_pa_kernel(tc, x, head_w_words, head_w_scales, head_b, cb_v, cb_g, 
                 )
             w4_words = inputs.tile([P, PASSES_IN, 2 * D_EMB], U8, name="w4_words", align_bytes=64)
             nc.sync.dma_start(out=w4_words[:].bitcast(I32), in_=head_w_words.bitcast(I32).rearrange("g p b -> p g b"))
+            bias_alone = inputs.tile([P, D_EMB], BF16, name="bias_alone")
+            nc.gpsimd.memset(bias_alone[:], 0.0)
+            nc.sync.dma_start(out=bias_alone[0:1, :], in_=head_b.rearrange("(r c) -> r c", r=1))
+            ones = inputs.tile([P, P], BF16, name="ones")
+            nc.gpsimd.memset(ones[:], 1.0)
 
             cb_sb = inputs.tile([P, K_TILES, D_EMB], BF16, name="cb_sb")
             cb_rows = cb_v.rearrange("(p t) c -> p t c", t=K_TILES)
             gain = inputs.tile([P, K_TILES], BF16, name="gain")
             bias_row = inputs.tile([P, D_EMB], BF16, name="bias_row")
+            bias_spread = []
 
             for first in range(0, ROW_TILES, GROUP):
                 view, t = first // S_TILES, first % S_TILES
                 loaded = 1 if first == 0 else 0
                 nc.sync.dma_start(out=x_sb[:, view, t + loaded : t + GROUP, :], in_=x_rows[view][:, t + loaded : t + GROUP, :])
                 if first == 0:
-                    nc.sync.dma_start(out=bias_row[:], in_=head_b.partition_broadcast(P))
                     nc.sync.dma_start(out=gain[:], in_=cb_g.rearrange("(p t) -> p t", t=K_TILES))
                 nc.sync.dma_start(out=cb_sb[:, first : first + GROUP, :], in_=cb_rows[:, first : first + GROUP, :])
 
@@ -216,6 +221,11 @@ def tile_spin_pa_kernel(tc, x, head_w_words, head_w_scales, head_b, cb_v, cb_g, 
                     for lag, step in reversed(list(enumerate(to_the_norms))):
                         if 0 <= now - lag < ROW_TILES:
                             step(now - lag)
+                    if now == 1:
+                        bias_spread.append(banks.tile([P, D_EMB], F32, tag="bank", name="bias_spread"))
+                        nc.tensor.matmul(out=bias_spread[0][:], lhsT=ones[:], rhs=bias_alone[:], start=True, stop=True)
+                    if now == 2:
+                        nc.vector.tensor_copy(out=bias_row[:], in_=bias_spread[0][:])
 
         matrix = ctx.enter_context(tc.tile_pool(name="matrix", bufs=1))
         work = ctx.enter_context(tc.tile_pool(name="work", bufs=2))

@@ -35,6 +35,9 @@ DIVIDE_LAG = 1
 ADD_LAG = 3
 CLOSE_LAG = 4
 RUN = 2
+C_PER_TICK = 2
+C_START = 2
+E_PER_TICK = 1
 
 FLOPS = 2 * VIEWS * SAMPLES * D_IN * D_EMB + 2 * VIEWS * SAMPLES * CODES * D_EMB
 
@@ -54,182 +57,9 @@ def tile_spin_pa_kernel(tc, x, head_w_words, head_w_scales, head_b, cb_v, cb_g, 
         w_codes = keep.tile([P, K_TILES, P], U32, name="w_codes", align_bytes=64)
         w_scales = keep.tile([P, K_TILES, P], U8, name="w_scales", align_bytes=64)
 
-        with tc.tile_pool(name="stage", bufs=3) as stage, tc.tile_pool(name="inputs", bufs=1) as inputs:
-            x_sb = inputs.tile([P, VIEWS, S_TILES, D_IN], BF16, name="x_sb")
-            x_rows = x.rearrange("(p t v) d -> v p t d", t=S_TILES, v=VIEWS)
-            nc.sync.dma_start(out=x_sb[:, 0, 0:1, :], in_=x_rows[0][:, 0:1, :])
-            w4_scales = inputs.tile([P, PASSES_IN, D_EMB], U8, name="w4_scales", align_bytes=64)
-            nc.vector.memset(w4_scales[:].bitcast(I32), 0)
-            for quadrant in range(4):
-                nc.sync.dma_start(
-                    out=w4_scales[32 * quadrant : 32 * quadrant + 4, :, :].bitcast(I32),
-                    in_=head_w_scales.bitcast(I32)[:, 4 * quadrant : 4 * quadrant + 4, :].rearrange("g r n -> r g n"),
-                )
-            w4_words = inputs.tile([P, PASSES_IN, 2 * D_EMB], U8, name="w4_words", align_bytes=64)
-            nc.sync.dma_start(out=w4_words[:].bitcast(I32), in_=head_w_words.bitcast(I32).rearrange("g p b -> p g b"))
-            bias_alone = inputs.tile([P, D_EMB], BF16, name="bias_alone")
-            nc.gpsimd.memset(bias_alone[:], 0.0)
-            nc.sync.dma_start(out=bias_alone[0:1, :], in_=head_b.rearrange("(r c) -> r c", r=1))
-            ones = inputs.tile([P, P], BF16, name="ones")
-            nc.gpsimd.memset(ones[:], 1.0)
-
-            cb_sb = inputs.tile([P, K_TILES, D_EMB], BF16, name="cb_sb")
-            cb_rows = cb_v.rearrange("(p t) c -> p t c", t=K_TILES)
-            gain = inputs.tile([P, K_TILES], BF16, name="gain")
-            bias_row = inputs.tile([P, D_EMB], BF16, name="bias_row")
-            bias_spread = []
-
-            for first in range(0, ROW_TILES, GROUP):
-                view, t = first // S_TILES, first % S_TILES
-                loaded = 1 if first == 0 else 0
-                nc.sync.dma_start(out=x_sb[:, view, t + loaded : t + GROUP, :], in_=x_rows[view][:, t + loaded : t + GROUP, :])
-                if first == 0:
-                    nc.sync.dma_start(out=gain[:], in_=cb_g.rearrange("(p t) -> p t", t=K_TILES))
-                nc.sync.dma_start(out=cb_sb[:, first : first + GROUP, :], in_=cb_rows[:, first : first + GROUP, :])
-
-            h_rows = inputs.tile([P, ROW_TILES, D_EMB], F32, name="h_rows")
-            h_square_sum = inputs.tile([P, ROW_TILES], F32, name="h_square_sum")
-            v_square_sum = inputs.tile([P, K_TILES], F32, name="v_square_sum")
-            x_turned = {}
-            x_grouped = {}
-            x_quantised = {}
-            h_sums = {}
-            norms = {}
-            normalised = {}
-            factors = {}
-            grouped = {}
-            turned = {}
-
-            def turn_x(i):
-                x_words = x_sb[:, i // S_TILES, i % S_TILES, :].bitcast(F32)
-                x_turned[i] = banks.tile([P, PASSES_IN, 2, P], F32, tag="bank", name="x_turned")
-                for g in range(PASSES_IN):
-                    for u in range(2):
-                        nc.tensor.transpose(
-                            x_turned[i][:, g, u, :], x_words[:, 256 * g + u : 256 * (g + 1) : 2], ident_f32[:]
-                        )
-
-            def lay_out_x(i):
-                x_grouped[i] = stage.tile([P, PASSES_IN, P, PACK], BF16, name="x_grouped", align_bytes=64)
-                nc.scalar.copy(out=x_grouped[i][:].bitcast(F32), in_=x_turned[i][:].rearrange("p g u s -> p g s u"))
-
-            def quantise_x(i):
-                x_codes = stage.tile([P, PASSES_IN, P], U32, name="x_codes", align_bytes=64)
-                x_scales = stage.tile([P, PASSES_IN, P], U8, name="x_scales", align_bytes=64)
-                nc.vector.quantize_mx(
-                    out=x_codes[:].rearrange("p g s -> p (g s)").bitcast(FP8X4),
-                    scales=x_scales[:].rearrange("p g s -> p (g s)"),
-                    in_=x_grouped[i][:].rearrange("p g s j -> p (g s j)"),
-                )
-                x_quantised[i] = (x_codes, x_scales)
-
-            def multiply_by_head(i):
-                x_codes, x_scales = x_quantised[i]
-                h_sums[i] = banks.tile([P, D_EMB], F32, tag="bank", name="h_sum")
-                for g in range(PASSES_IN):
-                    nc.tensor.matmul_mx(
-                        out=h_sums[i][:],
-                        lhsT=x_codes[:, g, :].bitcast(FP8X4),
-                        lhsT_scale=x_scales[:, g, :],
-                        rhs=w4_words[:, g, :].bitcast(FP4X4),
-                        rhs_scale=w4_scales[:, g, :],
-                        start=(g == 0),
-                        stop=(g == PASSES_IN - 1),
-                    )
-
-            def add_bias(i):
-                nc.vector.tensor_tensor(out=h_rows[:, i, :], in0=h_sums[i][:], in1=bias_row[:], op=ALU.add)
-
-            def square_rows(i):
-                for rows, square_sum in ((h_rows[:, i, :], h_square_sum), (cb_sb[:, i, :], v_square_sum)):
-                    squares = stage.tile([P, D_EMB], BF16, name="squares")
-                    nc.scalar.activation(out=squares[:], in_=rows, func=ACT.Square, accum_out=square_sum[:, i : i + 1])
-                if i % GROUP == GROUP - 1:
-                    tiles = slice(i + 1 - GROUP, i + 1)
-                    h_norm = small.tile([P, GROUP], F32, name="h_norm")
-                    nc.scalar.sqrt(out=h_norm[:], in_=h_square_sum[:, tiles])
-                    v_norm = small.tile([P, GROUP], F32, name="v_norm")
-                    nc.scalar.sqrt(out=v_norm[:], in_=v_square_sum[:, tiles])
-                    norms[i + 1 - GROUP] = (h_norm, v_norm)
-
-            def factors_of_group(first):
-                h_norm, v_norm = norms[first]
-                nc.vector.tensor_scalar_max(out=h_norm[:], in0=h_norm[:], scalar1=1e-12)
-                inv_v = small.tile([P, GROUP], F32, name="inv_v")
-                nc.vector.reciprocal(out=inv_v[:], in_=v_norm[:])
-                inv_h = small.tile([P, GROUP], F32, name="inv_h")
-                nc.vector.reciprocal(out=inv_h[:], in_=h_norm[:])
-                nc.vector.tensor_tensor(out=inv_v[:], in0=inv_v[:], in1=gain[:, first : first + GROUP], op=ALU.mult)
-                factors[first] = (inv_h, inv_v)
-                grouped[first] = (
-                    stage.tile([P, GROUP, P, PACK], BF16, name="hn_grouped", align_bytes=64),
-                    stage.tile([P, GROUP, P, PACK], BF16, name="w_grouped", align_bytes=64),
-                )
-
-            def normalise(i):
-                inv_h, gain_over_v = factors[i - i % GROUP]
-                slot = i % GROUP
-                hn_rows = stage.tile([P, D_EMB], BF16, name="hn_rows")
-                nc.vector.tensor_scalar_mul(out=hn_rows[:], in0=h_rows[:, i, :], scalar1=inv_h[:, slot : slot + 1])
-                w_rows = stage.tile([P, D_EMB], BF16, name="w_rows")
-                nc.vector.tensor_scalar_mul(out=w_rows[:], in0=cb_sb[:, i, :], scalar1=gain_over_v[:, slot : slot + 1])
-                normalised[i] = (hn_rows, w_rows)
-
-            def turn_rows(i):
-                turned[i] = []
-                for rows in normalised[i]:
-                    words = rows[:].bitcast(F32)
-                    columns = banks.tile([P, 2, P], F32, tag="bank", name="columns")
-                    for u in range(2):
-                        nc.tensor.transpose(columns[:, u, :], words[:, u * P : (u + 1) * P], ident_f32[:])
-                    turned[i].append(columns)
-
-            def lay_out_rows(i):
-                hn_grouped, w_grouped = grouped[i - i % GROUP]
-                hn_columns, w_columns = turned[i]
-                slot = i % GROUP
-                nc.scalar.copy(out=hn_grouped[:, slot, :, :].bitcast(F32), in_=hn_columns[:].rearrange("p u r -> p r u"))
-                nc.vector.tensor_copy(out=w_grouped[:, slot, :, :].bitcast(F32), in_=w_columns[:].rearrange("p u r -> p r u"))
-
-            def quantise_group(first):
-                hn_grouped, w_grouped = grouped[first]
-                view, t = first // S_TILES, first % S_TILES
-                nc.vector.quantize_mx(
-                    out=hn_codes[:, view, t * P : (t + GROUP) * P].bitcast(FP8X4),
-                    scales=hn_scales[:, view, t * P : (t + GROUP) * P],
-                    in_=hn_grouped[:].rearrange("p t s j -> p (t s j)"),
-                )
-                nc.vector.quantize_mx(
-                    out=w_codes[:, first : first + GROUP, :].rearrange("p t k -> p (t k)").bitcast(FP8X4),
-                    scales=w_scales[:, first : first + GROUP, :].rearrange("p t k -> p (t k)"),
-                    in_=w_grouped[:].rearrange("p t k j -> p (t k j)"),
-                )
-
-            to_the_norms = (turn_x, lay_out_x, quantise_x, multiply_by_head, add_bias, square_rows)
-            from_the_norms = (normalise, turn_rows, lay_out_rows)
-            factors_lag = len(to_the_norms) + GROUP - 1
-            quantise_lag = factors_lag + len(from_the_norms) + GROUP
-            with tc.manual_schedule():
-                for now in range(ROW_TILES - GROUP + quantise_lag + 1):
-                    if 0 <= now - quantise_lag < ROW_TILES and (now - quantise_lag) % GROUP == 0:
-                        quantise_group(now - quantise_lag)
-                    for lag, step in reversed(list(enumerate(from_the_norms))):
-                        if 0 <= now - factors_lag - 1 - lag < ROW_TILES:
-                            step(now - factors_lag - 1 - lag)
-                    if 0 <= now - factors_lag < ROW_TILES and (now - factors_lag) % GROUP == 0:
-                        factors_of_group(now - factors_lag)
-                    for lag, step in reversed(list(enumerate(to_the_norms))):
-                        if 0 <= now - lag < ROW_TILES:
-                            step(now - lag)
-                    if now == 1:
-                        bias_spread.append(banks.tile([P, D_EMB], F32, tag="bank", name="bias_spread"))
-                        nc.tensor.matmul(out=bias_spread[0][:], lhsT=ones[:], rhs=bias_alone[:], start=True, stop=True)
-                    if now == 2:
-                        nc.vector.tensor_copy(out=bias_row[:], in_=bias_spread[0][:])
-
-        matrix = ctx.enter_context(tc.tile_pool(name="matrix", bufs=1))
+        first_matrix = ctx.enter_context(tc.tile_pool(name="first_matrix", bufs=1))
         work = ctx.enter_context(tc.tile_pool(name="work", bufs=2))
-        e = [matrix.tile([P, K_TILES, SAMPLES], F32, name="e%d" % view) for view in range(VIEWS)]
+        e = [first_matrix.tile([P, K_TILES, SAMPLES], F32, name="e0"), None]
 
         def logits_by_code(kt, view, half):
             zt = banks.tile([P, BANK], F32, tag="bank")
@@ -474,28 +304,249 @@ def tile_spin_pa_kernel(tc, x, head_w_words, head_w_scales, head_b, cb_v, cb_g, 
                 op0=ALU.mult, op1=ALU.add,
             )
 
-        with tc.manual_schedule():
-            for now in range(len(units) + CLOSE_LAG):
+        def run_of_tiles(now, first_slot):
+            if first_slot == 0:
                 if now == len(units):
                     take_logarithms()
                 if now == len(units) + CLOSE_LAG - 1:
                     all_but_the_last_term()
                 if 0 <= now - CLOSE_LAG:
                     close_pass(now - CLOSE_LAG)
+            for slot in range(first_slot, first_slot + RUN):
+                if now < len(units):
+                    start_tile(now, slot, small_steps_of(now, slot))
+                else:
+                    small_steps_of(now, slot)()
+                if first_weigh_unit < now <= first_weigh_unit + SOFTMAX_PIECES // GROUP:
+                    softmax_piece((now - first_weigh_unit - 1) * GROUP + slot)
+            for slot in range(first_slot, first_slot + RUN):
+                if 0 <= now - ADD_LAG < len(units):
+                    add_tile_of_unit(now - ADD_LAG, slot)
+            if first_slot + RUN == GROUP and 0 <= now - DIVIDE_LAG < len(units):
+                invert_sums(now - DIVIDE_LAG)
+                divide_unit(now - DIVIDE_LAG)
+
+        with tc.tile_pool(name="stage", bufs=3) as stage, tc.tile_pool(name="inputs", bufs=1) as inputs:
+            x_sb = inputs.tile([P, VIEWS, S_TILES, D_IN], BF16, name="x_sb")
+            x_rows = x.rearrange("(p t v) d -> v p t d", t=S_TILES, v=VIEWS)
+            nc.sync.dma_start(out=x_sb[:, 0, 0:1, :], in_=x_rows[0][:, 0:1, :])
+            w4_scales = inputs.tile([P, PASSES_IN, D_EMB], U8, name="w4_scales", align_bytes=64)
+            nc.vector.memset(w4_scales[:].bitcast(I32), 0)
+            for quadrant in range(4):
+                nc.sync.dma_start(
+                    out=w4_scales[32 * quadrant : 32 * quadrant + 4, :, :].bitcast(I32),
+                    in_=head_w_scales.bitcast(I32)[:, 4 * quadrant : 4 * quadrant + 4, :].rearrange("g r n -> r g n"),
+                )
+            w4_words = inputs.tile([P, PASSES_IN, 2 * D_EMB], U8, name="w4_words", align_bytes=64)
+            nc.sync.dma_start(out=w4_words[:].bitcast(I32), in_=head_w_words.bitcast(I32).rearrange("g p b -> p g b"))
+            bias_alone = inputs.tile([P, D_EMB], BF16, name="bias_alone")
+            nc.gpsimd.memset(bias_alone[:], 0.0)
+            nc.sync.dma_start(out=bias_alone[0:1, :], in_=head_b.rearrange("(r c) -> r c", r=1))
+            ones = inputs.tile([P, P], BF16, name="ones")
+            nc.gpsimd.memset(ones[:], 1.0)
+
+            cb_sb = inputs.tile([P, K_TILES, D_EMB], BF16, name="cb_sb")
+            cb_rows = cb_v.rearrange("(p t) c -> p t c", t=K_TILES)
+            gain = inputs.tile([P, K_TILES], BF16, name="gain")
+            bias_row = inputs.tile([P, D_EMB], BF16, name="bias_row")
+            bias_spread = []
+
+            for n in range(1, ROW_TILES):
+                nc.sync.dma_start(out=x_sb[:, n // S_TILES, n % S_TILES : n % S_TILES + 1, :], in_=x_rows[n // S_TILES][:, n % S_TILES : n % S_TILES + 1, :])
+                if n == C_START:
+                    nc.sync.dma_start(out=gain[:], in_=cb_g.rearrange("(p t) -> p t", t=K_TILES))
+                first = (n - C_START) * C_PER_TICK
+                if 0 <= first < K_TILES:
+                    nc.sync.dma_start(out=cb_sb[:, first : first + C_PER_TICK, :], in_=cb_rows[:, first : first + C_PER_TICK, :])
+
+            h_rows = inputs.tile([P, ROW_TILES, D_EMB], F32, name="h_rows")
+            square_sum = [inputs.tile([P, ROW_TILES], F32, name="square_sum%d" % kind) for kind in range(2)]
+            x_turned = {}
+            x_grouped = {}
+            x_quantised = {}
+            h_sums = {}
+            norms = {}
+            factors = {}
+            normalised = {}
+            turned = {}
+            grouped = {}
+
+            def turn_x(i):
+                x_words = x_sb[:, i // S_TILES, i % S_TILES, :].bitcast(F32)
+                x_turned[i] = banks.tile([P, PASSES_IN, 2, P], F32, tag="bank", name="x_turned")
+                for g in range(PASSES_IN):
+                    for u in range(2):
+                        nc.tensor.transpose(
+                            x_turned[i][:, g, u, :], x_words[:, 256 * g + u : 256 * (g + 1) : 2], ident_f32[:]
+                        )
+
+            def lay_out_x(i):
+                x_grouped[i] = stage.tile([P, PASSES_IN, P, PACK], BF16, name="x_grouped", align_bytes=64)
+                nc.scalar.copy(out=x_grouped[i][:].bitcast(F32), in_=x_turned[i][:].rearrange("p g u s -> p g s u"))
+
+            def quantise_x(i):
+                x_codes = stage.tile([P, PASSES_IN, P], U32, name="x_codes", align_bytes=64)
+                x_scales = stage.tile([P, PASSES_IN, P], U8, name="x_scales", align_bytes=64)
+                nc.vector.quantize_mx(
+                    out=x_codes[:].rearrange("p g s -> p (g s)").bitcast(FP8X4),
+                    scales=x_scales[:].rearrange("p g s -> p (g s)"),
+                    in_=x_grouped[i][:].rearrange("p g s j -> p (g s j)"),
+                )
+                x_quantised[i] = (x_codes, x_scales)
+
+            def multiply_by_head(i):
+                x_codes, x_scales = x_quantised[i]
+                h_sums[i] = banks.tile([P, D_EMB], F32, tag="bank", name="h_sum")
+                for g in range(PASSES_IN):
+                    nc.tensor.matmul_mx(
+                        out=h_sums[i][:],
+                        lhsT=x_codes[:, g, :].bitcast(FP8X4),
+                        lhsT_scale=x_scales[:, g, :],
+                        rhs=w4_words[:, g, :].bitcast(FP4X4),
+                        rhs_scale=w4_scales[:, g, :],
+                        start=(g == 0),
+                        stop=(g == PASSES_IN - 1),
+                    )
+
+            def add_bias(i):
+                nc.vector.tensor_tensor(out=h_rows[:, i, :], in0=h_sums[i][:], in1=bias_row[:], op=ALU.add)
+
+            def rows_of(kind, i):
+                return h_rows[:, i, :] if kind == 0 else cb_sb[:, i, :]
+
+            def square(kind, i):
+                squares = stage.tile([P, D_EMB], BF16, name="squares")
+                nc.scalar.activation(
+                    out=squares[:], in_=rows_of(kind, i), func=ACT.Square, accum_out=square_sum[kind][:, i : i + 1]
+                )
+
+            def root(kind, first):
+                norms[(kind, first)] = small.tile([P, GROUP], F32, name="norm%d" % kind)
+                nc.scalar.sqrt(out=norms[(kind, first)][:], in_=square_sum[kind][:, first : first + GROUP])
+
+            def first_factor_step(kind, first):
+                norm = norms[(kind, first)]
+                if kind == 0:
+                    nc.vector.tensor_scalar_max(out=norm[:], in0=norm[:], scalar1=1e-12)
+                else:
+                    factors[(kind, first)] = small.tile([P, GROUP], F32, name="factor%d" % kind)
+                    nc.vector.reciprocal(out=factors[(kind, first)][:], in_=norm[:])
+
+            def second_factor_step(kind, first):
+                if kind == 0:
+                    factors[(kind, first)] = small.tile([P, GROUP], F32, name="factor%d" % kind)
+                    nc.vector.reciprocal(out=factors[(kind, first)][:], in_=norms[(kind, first)][:])
+                else:
+                    factor = factors[(kind, first)]
+                    nc.vector.tensor_tensor(out=factor[:], in0=factor[:], in1=gain[:, first : first + GROUP], op=ALU.mult)
+                grouped[(kind, first)] = stage.tile([P, GROUP, P, PACK], BF16, name="grouped%d" % kind, align_bytes=64)
+
+            def normalise(kind, i):
+                slot = i % GROUP
+                normalised[(kind, i)] = stage.tile([P, D_EMB], BF16, name="normalised%d" % kind)
+                NORMALISE(kind)(
+                    out=normalised[(kind, i)][:], in0=rows_of(kind, i), scalar1=factors[(kind, i - slot)][:, slot : slot + 1],
+                    scalar2=0.0, op0=ALU.mult, op1=ALU.add,
+                )
+
+            def turn(kind, i):
+                words = normalised[(kind, i)][:].bitcast(F32)
+                turned[(kind, i)] = banks.tile([P, 2, P], F32, tag="bank", name="turned")
+                for u in range(2):
+                    nc.tensor.transpose(turned[(kind, i)][:, u, :], words[:, u * P : (u + 1) * P], ident_f32[:])
+
+            def lay_out(kind, i):
+                slot = i % GROUP
+                COPY(kind)(
+                    out=grouped[(kind, i - slot)][:, slot, :, :].bitcast(F32), in_=turned[(kind, i)][:].rearrange("p u r -> p r u")
+                )
+
+            def quantise(kind, first):
+                if kind == 0:
+                    view, t = first // S_TILES, first % S_TILES
+                    codes, scales = hn_codes[:, view, t * P : (t + GROUP) * P], hn_scales[:, view, t * P : (t + GROUP) * P]
+                else:
+                    codes = w_codes[:, first : first + GROUP, :].rearrange("p t k -> p (t k)")
+                    scales = w_scales[:, first : first + GROUP, :].rearrange("p t k -> p (t k)")
+                nc.vector.quantize_mx(
+                    out=codes.bitcast(FP8X4), scales=scales, in_=grouped[(kind, first)][:].rearrange("p t s j -> p (t s j)")
+                )
+
+            def NORMALISE(kind):
+                return nc.vector.tensor_scalar
+
+            def COPY(kind):
+                return nc.scalar.copy if kind == 0 else nc.vector.tensor_copy
+
+            def tile_due(i):
+                return 0 <= i < ROW_TILES
+
+            def group_due(i):
+                return 0 <= i < ROW_TILES and i % GROUP == 0
+
+            def rows_tick(kind, n):
+                if group_due(n - 10 - GROUP):
+                    quantise(kind, n - 10 - GROUP)
+                if tile_due(n - GROUP - 4):
+                    lay_out(kind, n - GROUP - 4)
+                if tile_due(n - GROUP - 3):
+                    turn(kind, n - GROUP - 3)
+                if tile_due(n - GROUP - 2):
+                    normalise(kind, n - GROUP - 2)
+                if group_due(n - GROUP - 1):
+                    second_factor_step(kind, n - GROUP - 1)
+                if tile_due(n):
+                    square(kind, n)
+
+            def rows_tick_end(kind, n):
+                if group_due(n - GROUP):
+                    first_factor_step(kind, n - GROUP)
+                if group_due(n - GROUP + 1):
+                    root(kind, n - GROUP + 1)
+
+            to_the_squares = (turn_x, lay_out_x, quantise_x, multiply_by_head, add_bias)
+
+            def x_tick(n):
+                rows_tick(0, n - len(to_the_squares))
+                for lag, step in reversed(list(enumerate(to_the_squares))):
+                    if tile_due(n - lag):
+                        step(n - lag)
+                rows_tick_end(0, n - len(to_the_squares))
+
+            def c_tick(n):
+                rows_tick(1, n)
+                rows_tick_end(1, n)
+
+            rows_ticks = ROW_TILES + 10 + 1
+            x_ticks = rows_ticks + len(to_the_squares)
+            first_view_done = S_TILES + 10 + len(to_the_squares)
+            with tc.manual_schedule():
+                c_done = 0
+                e_done = 0
+                for n in range(x_ticks):
+                    x_tick(n)
+                    for repeat in range(C_PER_TICK):
+                        if n >= C_START and c_done < rows_ticks:
+                            c_tick(c_done)
+                            c_done += 1
+                    if n == 1:
+                        bias_spread.append(banks.tile([P, D_EMB], F32, tag="bank", name="bias_spread"))
+                        nc.tensor.matmul(out=bias_spread[0][:], lhsT=ones[:], rhs=bias_alone[:], start=True, stop=True)
+                    if n == 2:
+                        nc.vector.tensor_copy(out=bias_row[:], in_=bias_spread[0][:])
+                    if n > first_view_done:
+                        for repeat in range(E_PER_TICK):
+                            run_of_tiles(e_done // GROUP, e_done % GROUP)
+                            e_done += RUN
+                assert c_done == rows_ticks and e_done % GROUP == 0
+
+        second_matrix = ctx.enter_context(tc.tile_pool(name="second_matrix", bufs=1))
+        e[1] = second_matrix.tile([P, K_TILES, SAMPLES], F32, name="e1")
+
+        with tc.manual_schedule():
+            for now in range(e_done // GROUP, len(units) + CLOSE_LAG):
                 for first_slot in range(0, GROUP, RUN):
-                    for slot in range(first_slot, first_slot + RUN):
-                        if now < len(units):
-                            start_tile(now, slot, small_steps_of(now, slot))
-                        else:
-                            small_steps_of(now, slot)()
-                        if first_weigh_unit < now <= first_weigh_unit + SOFTMAX_PIECES // GROUP:
-                            softmax_piece((now - first_weigh_unit - 1) * GROUP + slot)
-                    for slot in range(first_slot, first_slot + RUN):
-                        if 0 <= now - ADD_LAG < len(units):
-                            add_tile_of_unit(now - ADD_LAG, slot)
-                if 0 <= now - DIVIDE_LAG < len(units):
-                    invert_sums(now - DIVIDE_LAG)
-                    divide_unit(now - DIVIDE_LAG)
+                    run_of_tiles(now, first_slot)
 
             last_logit = small.tile([P, S_TILES], F32, name="last_logit")
             nc.vector.tensor_tensor(out=last_logit[:], in0=dot_sum[1][:], in1=inv_last[1][:], op=ALU.mult)

@@ -473,7 +473,7 @@ def tile_spin_pa_kernel(tc, x, head_w_words, head_w_scales, head_b, cb_v, cb_g, 
                 )
 
             def NORMALISE(kind):
-                return nc.vector.tensor_scalar
+                return nc.gpsimd.tensor_scalar
 
             def COPY(kind):
                 return nc.scalar.copy if kind == 0 else nc.vector.tensor_copy

from contextlib import ExitStack

import concourse.mybir as mybir
from concourse.masks import make_identity

F32 = mybir.dt.float32
BF16 = mybir.dt.bfloat16
I32 = mybir.dt.int32
U32 = mybir.dt.uint32
U8 = mybir.dt.uint8
FP8X4 = mybir.dt.float8_e4m3fn_x4
FP4X4 = mybir.dt.float4_e2m1fn_x4
ALU = mybir.AluOpType
ACT = mybir.ActivationFunctionType
AX = mybir.AxisListType

P = 128
PACK = 4
BANK = 512
VIEWS = 2
D_IN = 1024
PASSES_IN = D_IN // (P * PACK)
D_EMB = 512
SAMPLES = 1024
S_TILES = SAMPLES // P
CODES = 2048
K_TILES = CODES // P
ROW_TILES = VIEWS * S_TILES
assert ROW_TILES == K_TILES
GROUP = 4
INV_EPSILON = 50.0
INV_TEMPERATURE = 10.0
MORE_ROUNDS = 2
DIVIDE_LAG = 1
ADD_LAG = 3
CLOSE_LAG = 4
RUN = 2
C_PER_TICK = 2
C_START = 2
E_PER_TICK = 1

FLOPS = 2 * VIEWS * SAMPLES * D_IN * D_EMB + 2 * VIEWS * SAMPLES * CODES * D_EMB


def tile_spin_pa_kernel(tc, x, head_w_words, head_w_scales, head_b, cb_v, cb_g, out):
    nc = tc.nc
    with ExitStack() as ctx:
        keep = ctx.enter_context(tc.tile_pool(name="keep", bufs=1))
        small = ctx.enter_context(tc.tile_pool(name="small", bufs=4))
        banks = ctx.enter_context(tc.psum_pool(name="banks", bufs=8))

        ident_f32 = keep.tile([P, P], F32, name="ident_f32")
        make_identity(nc, ident_f32[:])

        hn_codes = keep.tile([P, VIEWS, SAMPLES], U32, name="hn_codes", align_bytes=64)
        hn_scales = keep.tile([P, VIEWS, SAMPLES], U8, name="hn_scales", align_bytes=64)
        w_codes = keep.tile([P, K_TILES, P], U32, name="w_codes", align_bytes=64)
        w_scales = keep.tile([P, K_TILES, P], U8, name="w_scales", align_bytes=64)

        first_matrix = ctx.enter_context(tc.tile_pool(name="first_matrix", bufs=1))
        work = ctx.enter_context(tc.tile_pool(name="work", bufs=2))
        e = [first_matrix.tile([P, K_TILES, SAMPLES], F32, name="e0"), None]

        def logits_by_code(kt, view, half):
            zt = banks.tile([P, BANK], F32, tag="bank")
            columns = slice(half * BANK, (half + 1) * BANK)
            nc.tensor.matmul_mx(
                out=zt[:],
                lhsT=w_codes[:, kt, :].bitcast(FP8X4),
                lhsT_scale=w_scales[:, kt, :],
                rhs=hn_codes[:, view, columns].bitcast(FP8X4),
                rhs_scale=hn_scales[:, view, columns],
                start=True,
                stop=True,
            )
            return zt, columns

        def new_sample_sums():
            return [banks.tile([P, GROUP, P], F32, tag="bank", name="added%d" % i) for i in range(S_TILES // GROUP)]

        def add_code_tile(added, view, kt, last_kt):
            for t in range(S_TILES):
                nc.tensor.matmul(
                    out=added[t // GROUP][:, t % GROUP, :], lhsT=e[view][:, kt, t * P : (t + 1) * P], rhs=ident_f32[:],
                    is_transpose=True,
                    start=(kt == 0 and t % GROUP == 0), stop=(kt == last_kt and t % GROUP == GROUP - 1),
                )

        def finish_sample_sums(added):
            sums = small.tile([P, S_TILES], F32, name="sums", bufs=8)
            for i, bank in enumerate(added):
                nc.vector.tensor_reduce(out=sums[:, i * GROUP : (i + 1) * GROUP], in_=bank[:], axis=AX.X, op=ALU.add)
            return sums

        units = []
        for view in range(VIEWS):
            units.extend([("exp", view, first, "weigh") for first in range(0, K_TILES, GROUP)])
        for rounds_left in reversed(range(MORE_ROUNDS)):
            for view in range(VIEWS):
                then = "weigh" if rounds_left > 0 else "dot"
                units.extend([("weigh", view, first, then) for first in range(0, K_TILES, GROUP)])
        for view in range(VIEWS):
            units.extend([("dot", view, first, "end") for first in range(0, K_TILES, GROUP)])
        first_weigh_unit = VIEWS * K_TILES // GROUP
        SOFTMAX_PIECES = VIEWS * S_TILES * (CODES // BANK)

        shift = keep.tile([P, VIEWS, K_TILES], F32, name="shift")
        soft_shift = keep.tile([P, 1], F32, name="soft_shift")
        exp_part = keep.tile([P, VIEWS, S_TILES, CODES // BANK], F32, name="exp_part")
        part_sums = {}
        added = [None, None]
        weight_row = [None, None]
        last_sum = [None, None]
        dot_sum = [None, None]

        waiting_exp = []

        def exp_of_waiting_tile():
            for number, slot, halves, top in waiting_exp:
                kind, view, first, then = units[number]
                kt = first + slot
                nc.vector.tensor_scalar(
                    out=shift[:, view, kt : kt + 1], in0=top[:, 0:1], scalar1=top[:, 1:2], scalar2=-INV_EPSILON,
                    op0=ALU.max, op1=ALU.mult,
                )
                for half, (zt, columns) in enumerate(halves):
                    nc.scalar.activation(
                        out=e[view][:, kt, columns], in_=zt[:], func=ACT.Exp,
                        bias=shift[:, view, kt : kt + 1], scale=INV_EPSILON,
                        accum_out=part_sums[number][:, slot, half : half + 1],
                    )
            waiting_exp.clear()

        def start_tile(number, slot, small_steps):
            kind, view, first, then = units[number]
            if kind != "dot" and slot == 0:
                part_sums[number] = small.tile([P, GROUP, 2], F32, name="part_sum", bufs=4)
            kt = first + slot
            if kind == "exp":
                halves = [logits_by_code(kt, view, half) for half in range(2)]
                top = small.tile([P, 2], F32, name="top")
                for half, (zt, columns) in enumerate(halves):
                    nc.vector.tensor_reduce(out=top[:, half : half + 1], in_=zt[:], axis=AX.X, op=ALU.max)
                    if half == 0:
                        small_steps()
                waiting_exp.append((number, slot, halves, top))
            elif kind == "weigh":
                for half in range(2):
                    products = work.tile([P, BANK], F32, name="products")
                    nc.vector.scalar_tensor_tensor(
                        out=products[:], in0=e[view][:, kt, half * BANK : (half + 1) * BANK], scalar=1.0,
                        in1=weight_row[view][half][:].rearrange("p t m -> p (t m)"), op0=ALU.mult, op1=ALU.mult,
                        accum_out=part_sums[number][:, slot, half : half + 1],
                    )
                    if half == 0:
                        small_steps()
            else:
                for half in range(2):
                    zt, columns = logits_by_code(kt, 1 - view, half)
                    nc.vector.tensor_tensor(
                        out=e[view][:, kt, columns], in0=zt[:], in1=e[view][:, kt, columns], op=ALU.mult
                    )
                    if half == 0:
                        small_steps()

        code_sums = {}
        inv_codes = {}

        def add_halves(number):
            if units[number][0] != "dot":
                code_sums[number] = small.tile([P, GROUP], F32, name="code_sum")
                nc.vector.tensor_reduce(out=code_sums[number][:], in_=part_sums[number][:], axis=AX.X, op=ALU.add)

        def invert_sums(number):
            if units[number][0] != "dot":
                inv_codes[number] = small.tile([P, GROUP], F32, name="inv_code")
                nc.vector.reciprocal(out=inv_codes[number][:], in_=code_sums[number][:])

        def divide_unit(number):
            kind, view, first, then = units[number]
            if kind == "dot":
                if number < len(units) - 1:
                    for kt in range(first, first + GROUP, 2):
                        nc.gpsimd.tensor_tensor(
                            out=e[view][:, kt, :], in0=e[view][:, kt, :], in1=e[view][:, kt + 1, :], op=ALU.add
                        )
                return
            inv_code = inv_codes[number]
            for slot in range(GROUP):
                kt = first + slot
                if kind == "weigh" and kt % 2 == 0:
                    nc.scalar.activation(
                        out=e[view][:, kt, :], in_=e[view][:, kt, :], func=ACT.Copy, scale=inv_code[:, slot : slot + 1]
                    )
                else:
                    nc.gpsimd.tensor_scalar(
                        out=e[view][:, kt, :], in0=e[view][:, kt, :], scalar1=inv_code[:, slot : slot + 1], scalar2=0.0,
                        op0=ALU.mult, op1=ALU.add,
                    )

        def softmax_piece(piece):
            chunk = piece % (CODES // BANK)
            t = (piece // (CODES // BANK)) % S_TILES
            view = piece // (CODES // BANK * S_TILES)
            z = banks.tile([P, BANK], F32, tag="bank")
            tiles = slice(chunk * GROUP, (chunk + 1) * GROUP)
            nc.tensor.matmul_mx(
                out=z[:],
                lhsT=hn_codes[:, view, t * P : (t + 1) * P].bitcast(FP8X4),
                lhsT_scale=hn_scales[:, view, t * P : (t + 1) * P],
                rhs=w_codes[:, tiles, :].rearrange("p t k -> p (t k)").bitcast(FP8X4),
                rhs_scale=w_scales[:, tiles, :].rearrange("p t k -> p (t k)"),
                start=True,
                stop=True,
            )
            powers = work.tile([P, BANK], BF16, name="powers")
            nc.scalar.activation(
                out=powers[:], in_=z[:], func=ACT.Exp, bias=soft_shift[:], scale=INV_TEMPERATURE,
                accum_out=exp_part[:, view, t, chunk : chunk + 1],
            )

        def add_tile_of_unit(number, slot):
            kind, view, first, then = units[number]
            if first + slot == 0:
                added[view] = new_sample_sums()
            if kind != "dot" or number == len(units) - 1:
                add_code_tile(added[view], view, first + slot, K_TILES - 1)
            elif slot % 2 == 0:
                add_code_tile(added[view], view, first + slot, K_TILES - 1 if view == VIEWS - 1 else K_TILES - 2)

        def close_pass(number):
            kind, view, first, then = units[number]
            if first != K_TILES - GROUP:
                return
            sums = finish_sample_sums(added[view])
            if then == "dot":
                last_sum[view] = sums
            elif then == "end":
                dot_sum[view] = sums
            else:
                waiting_weights.append((view, sums))

        waiting_weights = []

        def weights_of_waiting_view():
            for view, sums in waiting_weights:
                weight = small.tile([P, S_TILES], F32, name="weight")
                nc.vector.reciprocal(out=weight[:], in_=sums[:])
                weight_row[view] = [banks.tile([P, GROUP, P], F32, tag="bank", name="row%d" % i) for i in range(2)]
                for t in range(S_TILES):
                    nc.tensor.transpose(
                        weight_row[view][t // GROUP][:, t % GROUP, :], weight[:, t : t + 1].to_broadcast([P, P]),
                        ident_f32[:],
                    )
            waiting_weights.clear()

        least = small.tile([P, 1], F32, name="least")
        least_of_all = small.tile([P, 1], F32, name="least_of_all")
        least_turned = []

        def soft_shift_step(step):
            if step == 1:
                nc.vector.tensor_reduce(out=least[:], in_=shift[:].rearrange("p v k -> p (v k)"), axis=AX.X, op=ALU.min)
                least_turned.append(banks.tile([P, P], F32, tag="bank", name="least_turned"))
                nc.tensor.transpose(least_turned[0][:], least[:].to_broadcast([P, P]), ident_f32[:])
            elif step == 2:
                nc.vector.tensor_reduce(out=least_of_all[:], in_=least_turned[0][:], axis=AX.X, op=ALU.min)
            elif step == 3:
                nc.vector.tensor_scalar_mul(out=soft_shift[:], in0=least_of_all[:], scalar1=INV_TEMPERATURE / INV_EPSILON)

        def small_steps_of(now, slot):
            def small_steps():
                exp_of_waiting_tile()
                if slot == GROUP - 2:
                    weights_of_waiting_view()
                if now == first_weigh_unit:
                    soft_shift_step(slot)
                if slot == GROUP - 1 and 0 <= now - DIVIDE_LAG < len(units):
                    add_halves(now - DIVIDE_LAG)

            return small_steps

        log_sum = small.tile([P, VIEWS, S_TILES], F32, name="log_sum")
        inv_last = [small.tile([P, S_TILES], F32, name="inv_last%d" % view) for view in range(VIEWS)]
        all_but_last = small.tile([P, S_TILES], F32, name="all_but_last")

        def take_logarithms():
            exp_sum = small.tile([P, VIEWS, S_TILES], F32, name="exp_sum")
            nc.vector.tensor_reduce(out=exp_sum[:], in_=exp_part[:], axis=AX.X, op=ALU.add)
            nc.scalar.activation(out=log_sum[:], in_=exp_sum[:], func=ACT.Ln)

        def all_but_the_last_term():
            both_logs = small.tile([P, S_TILES], F32, name="both_logs")
            nc.vector.tensor_tensor(out=both_logs[:], in0=log_sum[:, 0, :], in1=log_sum[:, 1, :], op=ALU.add)
            for view in range(VIEWS):
                nc.vector.reciprocal(out=inv_last[view][:], in_=last_sum[view][:])
            nc.vector.tensor_scalar(
                out=both_logs[:], in0=both_logs[:], scalar1=0.5, scalar2=soft_shift[:], op0=ALU.mult, op1=ALU.subtract
            )
            first_logit = small.tile([P, S_TILES], F32, name="first_logit")
            nc.vector.tensor_tensor(out=first_logit[:], in0=dot_sum[0][:], in1=inv_last[0][:], op=ALU.mult)
            nc.vector.scalar_tensor_tensor(
                out=all_but_last[:], in0=first_logit[:], scalar=-0.5 * INV_TEMPERATURE, in1=both_logs[:],
                op0=ALU.mult, op1=ALU.add,
            )

        def run_of_tiles(now, first_slot):
            if first_slot == 0:
                if now == len(units):
                    take_logarithms()
                if now == len(units) + CLOSE_LAG - 1:
                    all_but_the_last_term()
                if 0 <= now - CLOSE_LAG:
                    close_pass(now - CLOSE_LAG)
            for slot in range(first_slot, first_slot + RUN):
                if now < len(units):
                    start_tile(now, slot, small_steps_of(now, slot))
                else:
                    small_steps_of(now, slot)()
                if first_weigh_unit < now <= first_weigh_unit + SOFTMAX_PIECES // GROUP:
                    softmax_piece((now - first_weigh_unit - 1) * GROUP + slot)
            for slot in range(first_slot, first_slot + RUN):
                if 0 <= now - ADD_LAG < len(units):
                    add_tile_of_unit(now - ADD_LAG, slot)
            if first_slot + RUN == GROUP and 0 <= now - DIVIDE_LAG < len(units):
                invert_sums(now - DIVIDE_LAG)
                divide_unit(now - DIVIDE_LAG)

        with tc.tile_pool(name="stage", bufs=3) as stage, tc.tile_pool(name="inputs", bufs=1) as inputs:
            x_sb = inputs.tile([P, VIEWS, S_TILES, D_IN], BF16, name="x_sb")
            x_rows = x.rearrange("(p t v) d -> v p t d", t=S_TILES, v=VIEWS)
            nc.sync.dma_start(out=x_sb[:, 0, 0:1, :], in_=x_rows[0][:, 0:1, :])
            w4_scales = inputs.tile([P, PASSES_IN, D_EMB], U8, name="w4_scales", align_bytes=64)
            nc.vector.memset(w4_scales[:].bitcast(I32), 0)
            for quadrant in range(4):
                nc.sync.dma_start(
                    out=w4_scales[32 * quadrant : 32 * quadrant + 4, :, :].bitcast(I32),
                    in_=head_w_scales.bitcast(I32)[:, 4 * quadrant : 4 * quadrant + 4, :].rearrange("g r n -> r g n"),
                )
            w4_words = inputs.tile([P, PASSES_IN, 2 * D_EMB], U8, name="w4_words", align_bytes=64)
            nc.sync.dma_start(out=w4_words[:].bitcast(I32), in_=head_w_words.bitcast(I32).rearrange("g p b -> p g b"))
            bias_alone = inputs.tile([P, D_EMB], BF16, name="bias_alone")
            nc.gpsimd.memset(bias_alone[:], 0.0)
            nc.sync.dma_start(out=bias_alone[0:1, :], in_=head_b.rearrange("(r c) -> r c", r=1))
            ones = inputs.tile([P, P], BF16, name="ones")
            nc.gpsimd.memset(ones[:], 1.0)

            cb_sb = inputs.tile([P, K_TILES, D_EMB], BF16, name="cb_sb")
            cb_rows = cb_v.rearrange("(p t) c -> p t c", t=K_TILES)
            gain = inputs.tile([P, K_TILES], BF16, name="gain")
            bias_row = inputs.tile([P, D_EMB], BF16, name="bias_row")
            bias_spread = []

            for n in range(1, ROW_TILES):
                nc.sync.dma_start(out=x_sb[:, n // S_TILES, n % S_TILES : n % S_TILES + 1, :], in_=x_rows[n // S_TILES][:, n % S_TILES : n % S_TILES + 1, :])
                if n == C_START:
                    nc.sync.dma_start(out=gain[:], in_=cb_g.rearrange("(p t) -> p t", t=K_TILES))
                first = (n - C_START) * C_PER_TICK
                if 0 <= first < K_TILES:
                    nc.sync.dma_start(out=cb_sb[:, first : first + C_PER_TICK, :], in_=cb_rows[:, first : first + C_PER_TICK, :])

            h_rows = inputs.tile([P, ROW_TILES, D_EMB], F32, name="h_rows")
            square_sum = [inputs.tile([P, ROW_TILES], F32, name="square_sum%d" % kind) for kind in range(2)]
            x_turned = {}
            x_grouped = {}
            x_quantised = {}
            h_sums = {}
            norms = {}
            factors = {}
            normalised = {}
            turned = {}
            grouped = {}

            def turn_x(i):
                x_words = x_sb[:, i // S_TILES, i % S_TILES, :].bitcast(F32)
                x_turned[i] = banks.tile([P, PASSES_IN, 2, P], F32, tag="bank", name="x_turned")
                for g in range(PASSES_IN):
                    for u in range(2):
                        nc.tensor.transpose(
                            x_turned[i][:, g, u, :], x_words[:, 256 * g + u : 256 * (g + 1) : 2], ident_f32[:]
                        )

            def lay_out_x(i):
                x_grouped[i] = stage.tile([P, PASSES_IN, P, PACK], BF16, name="x_grouped", align_bytes=64)
                nc.scalar.copy(out=x_grouped[i][:].bitcast(F32), in_=x_turned[i][:].rearrange("p g u s -> p g s u"))

            def quantise_x(i):
                x_codes = stage.tile([P, PASSES_IN, P], U32, name="x_codes", align_bytes=64)
                x_scales = stage.tile([P, PASSES_IN, P], U8, name="x_scales", align_bytes=64)
                nc.vector.quantize_mx(
                    out=x_codes[:].rearrange("p g s -> p (g s)").bitcast(FP8X4),
                    scales=x_scales[:].rearrange("p g s -> p (g s)"),
                    in_=x_grouped[i][:].rearrange("p g s j -> p (g s j)"),
                )
                x_quantised[i] = (x_codes, x_scales)

            def multiply_by_head(i):
                x_codes, x_scales = x_quantised[i]
                h_sums[i] = banks.tile([P, D_EMB], F32, tag="bank", name="h_sum")
                for g in range(PASSES_IN):
                    nc.tensor.matmul_mx(
                        out=h_sums[i][:],
                        lhsT=x_codes[:, g, :].bitcast(FP8X4),
                        lhsT_scale=x_scales[:, g, :],
                        rhs=w4_words[:, g, :].bitcast(FP4X4),
                        rhs_scale=w4_scales[:, g, :],
                        start=(g == 0),
                        stop=(g == PASSES_IN - 1),
                    )

            def add_bias(i):
                nc.vector.tensor_tensor(out=h_rows[:, i, :], in0=h_sums[i][:], in1=bias_row[:], op=ALU.add)

            def rows_of(kind, i):
                return h_rows[:, i, :] if kind == 0 else cb_sb[:, i, :]

            def square(kind, i):
                squares = stage.tile([P, D_EMB], BF16, name="squares")
                nc.scalar.activation(
                    out=squares[:], in_=rows_of(kind, i), func=ACT.Square, accum_out=square_sum[kind][:, i : i + 1]
                )

            def root(kind, first):
                norms[(kind, first)] = small.tile([P, GROUP], F32, name="norm%d" % kind)
                nc.scalar.sqrt(out=norms[(kind, first)][:], in_=square_sum[kind][:, first : first + GROUP])

            def first_factor_step(kind, first):
                norm = norms[(kind, first)]
                if kind == 0:
                    nc.vector.tensor_scalar_max(out=norm[:], in0=norm[:], scalar1=1e-12)
                else:
                    factors[(kind, first)] = small.tile([P, GROUP], F32, name="factor%d" % kind)
                    nc.vector.reciprocal(out=factors[(kind, first)][:], in_=norm[:])

            def second_factor_step(kind, first):
                if kind == 0:
                    factors[(kind, first)] = small.tile([P, GROUP], F32, name="factor%d" % kind)
                    nc.vector.reciprocal(out=factors[(kind, first)][:], in_=norms[(kind, first)][:])
                else:
                    factor = factors[(kind, first)]
                    nc.vector.tensor_tensor(out=factor[:], in0=factor[:], in1=gain[:, first : first + GROUP], op=ALU.mult)
                grouped[(kind, first)] = stage.tile([P, GROUP, P, PACK], BF16, name="grouped%d" % kind, align_bytes=64)

            def normalise(kind, i):
                slot = i % GROUP
                normalised[(kind, i)] = stage.tile([P, D_EMB], BF16, name="normalised%d" % kind)
                NORMALISE(kind)(
                    out=normalised[(kind, i)][:], in0=rows_of(kind, i), scalar1=factors[(kind, i - slot)][:, slot : slot + 1],
                    scalar2=0.0, op0=ALU.mult, op1=ALU.add,
                )

            def turn(kind, i):
                words = normalised[(kind, i)][:].bitcast(F32)
                turned[(kind, i)] = banks.tile([P, 2, P], F32, tag="bank", name="turned")
                for u in range(2):
                    nc.tensor.transpose(turned[(kind, i)][:, u, :], words[:, u * P : (u + 1) * P], ident_f32[:])

            def lay_out(kind, i):
                slot = i % GROUP
                COPY(kind)(
                    out=grouped[(kind, i - slot)][:, slot, :, :].bitcast(F32), in_=turned[(kind, i)][:].rearrange("p u r -> p r u")
                )

            def quantise(kind, first):
                if kind == 0:
                    view, t = first // S_TILES, first % S_TILES
                    codes, scales = hn_codes[:, view, t * P : (t + GROUP) * P], hn_scales[:, view, t * P : (t + GROUP) * P]
                else:
                    codes = w_codes[:, first : first + GROUP, :].rearrange("p t k -> p (t k)")
                    scales = w_scales[:, first : first + GROUP, :].rearrange("p t k -> p (t k)")
                nc.vector.quantize_mx(
                    out=codes.bitcast(FP8X4), scales=scales, in_=grouped[(kind, first)][:].rearrange("p t s j -> p (t s j)")
                )

            def NORMALISE(kind):
                return nc.gpsimd.tensor_scalar

            def COPY(kind):
                return nc.scalar.copy if kind == 0 else nc.vector.tensor_copy

            def tile_due(i):
                return 0 <= i < ROW_TILES

            def group_due(i):
                return 0 <= i < ROW_TILES and i % GROUP == 0

            def rows_tick(kind, n):
                if group_due(n - 10 - GROUP):
                    quantise(kind, n - 10 - GROUP)
                if tile_due(n - GROUP - 4):
                    lay_out(kind, n - GROUP - 4)
                if tile_due(n - GROUP - 3):
                    turn(kind, n - GROUP - 3)
                if tile_due(n - GROUP - 2):
                    normalise(kind, n - GROUP - 2)
                if group_due(n - GROUP - 1):
                    second_factor_step(kind, n - GROUP - 1)
                if tile_due(n):
                    square(kind, n)

            def rows_tick_end(kind, n):
                if group_due(n - GROUP):
                    first_factor_step(kind, n - GROUP)
                if group_due(n - GROUP + 1):
                    root(kind, n - GROUP + 1)

            to_the_squares = (turn_x, lay_out_x, quantise_x, multiply_by_head, add_bias)

            def x_tick(n):
                rows_tick(0, n - len(to_the_squares))
                for lag, step in reversed(list(enumerate(to_the_squares))):
                    if tile_due(n - lag):
                        step(n - lag)
                rows_tick_end(0, n - len(to_the_squares))

            def c_tick(n):
                rows_tick(1, n)
                rows_tick_end(1, n)

            rows_ticks = ROW_TILES + 10 + 1
            x_ticks = rows_ticks + len(to_the_squares)
            first_view_done = S_TILES + 10 + len(to_the_squares)
            with tc.manual_schedule():
                c_done = 0
                e_done = 0
                for n in range(x_ticks):
                    x_tick(n)
                    for repeat in range(C_PER_TICK):
                        if n >= C_START and c_done < rows_ticks:
                            c_tick(c_done)
                            c_done += 1
                    if n == 1:
                        bias_spread.append(banks.tile([P, D_EMB], F32, tag="bank", name="bias_spread"))
                        nc.tensor.matmul(out=bias_spread[0][:], lhsT=ones[:], rhs=bias_alone[:], start=True, stop=True)
                    if n == 2:
                        nc.vector.tensor_copy(out=bias_row[:], in_=bias_spread[0][:])
                    if n > first_view_done:
                        for repeat in range(E_PER_TICK):
                            run_of_tiles(e_done // GROUP, e_done % GROUP)
                            e_done += RUN
                assert c_done == rows_ticks and e_done % GROUP == 0

        second_matrix = ctx.enter_context(tc.tile_pool(name="second_matrix", bufs=1))
        e[1] = second_matrix.tile([P, K_TILES, SAMPLES], F32, name="e1")

        with tc.manual_schedule():
            for now in range(e_done // GROUP, len(units) + CLOSE_LAG):
                for first_slot in range(0, GROUP, RUN):
                    run_of_tiles(now, first_slot)

            last_logit = small.tile([P, S_TILES], F32, name="last_logit")
            nc.vector.tensor_tensor(out=last_logit[:], in0=dot_sum[1][:], in1=inv_last[1][:], op=ALU.mult)
            loss = small.tile([P, S_TILES], F32, name="loss")
            nc.vector.scalar_tensor_tensor(
                out=loss[:], in0=last_logit[:], scalar=-0.5 * INV_TEMPERATURE, in1=all_but_last[:], op0=ALU.mult, op1=ALU.add
            )
            nc.sync.dma_start(out=out.rearrange("(p t) -> p t", t=S_TILES), in_=loss[:])
